import numpy as np
import ml_dtypes


def mxq(x, axis, fmt="e4m3"):
    dtype, down = {"e4m3": (ml_dtypes.float8_e4m3fn, 7), "e5m2": (ml_dtypes.float8_e5m2, 14)}[fmt]
    v = np.moveaxis(np.asarray(x, np.float32).astype(ml_dtypes.bfloat16).astype(np.float64), axis, -1)
    blocks = v.reshape(v.shape[:-1] + (-1, 32))
    amax = np.abs(blocks).max(-1, keepdims=True)
    byte = np.maximum(np.where(amax > 0, np.frexp(amax)[1] - 1 + 127, 0) - down, 1)
    scale = np.exp2(byte - 127.0)
    codes = (blocks / scale).astype(np.float32).astype(dtype).astype(np.float64)
    return np.moveaxis((codes * scale).reshape(v.shape), -1, axis)


WIDE = False


def mx_kscale(k):
    if not WIDE:
        return np.ones(k)
    levels = np.array([10, -10, 5, -5, 0])
    a = np.random.permutation(np.resize(levels, k // 512 * 4)).reshape(k // 512, 4)
    idx = np.arange(k)
    return np.exp2(a[idx // 512, idx % 128 // 32])


BF16 = ml_dtypes.bfloat16


def bf(x):
    return np.asarray(x, np.float32).astype(BF16)


def f64(x):
    return np.asarray(x).astype(np.float64)


B, HP, WP, E, F, NH, WS = 2, 32, 40, 512, 2048, 16, 8
NWH, NWW = HP // WS, WP // WS
L, N = B * NWH * NWW, WS * WS
LN_EPS = 1e-5
ERF_TERMS = 100


def erf(z):
    z = np.clip(z, -6.0, 6.0)
    u = z * z
    c = np.cumprod(np.concatenate([[1.0], 2.0 / (2.0 * np.arange(1, ERF_TERMS) + 1.0)]))
    acc = np.full_like(u, c[-1])
    for cn in c[-2::-1]:
        acc *= u
        acc += cn
    return 2.0 / np.sqrt(np.pi) * z * np.exp(-u) * acc


def gelu(v):
    return 0.5 * v * (1.0 + erf(v / np.sqrt(2.0)))


def layernorm(x, g, b):
    mu = x.mean(-1, keepdims=True)
    var = ((x - mu) ** 2).mean(-1, keepdims=True)
    return (x - mu) / np.sqrt(var + LN_EPS) * g + b


def setup_inputs():
    s = mx_kscale(E)
    s = s / s.max()
    return {"y": bf(np.random.standard_normal((L, N, E)) * s),
            "w1": bf(np.random.standard_normal((F, E)) / np.sqrt(E) / s),
            "b1": bf(np.random.standard_normal(F) * 0.2),
            "w2": bf(np.random.standard_normal((E, F)) * 1.5 / np.sqrt(F)),
            "b2": bf(np.random.standard_normal(E) * 0.2),
            "ln2_g": bf(1.0 + 0.1 * np.random.standard_normal(E)),
            "ln2_b": bf(np.random.standard_normal(E) * 0.2)}


def reference(y, w1, b1, w2, b2, ln2_g, ln2_b):
    y = f64(y)
    h = gelu((mxq(y, 2, "e4m3") @ mxq(f64(w1), 1, "e4m3").T) + f64(b1))
    ffn = (mxq(h, 2, "e4m3") @ mxq(f64(w2), 1, "e4m3").T) + f64(b2)
    z = layernorm(y + ffn, f64(ln2_g), f64(ln2_b))
    z = z.reshape(B, NWH, NWW, WS, WS, E).transpose(0, 1, 3, 2, 4, 5)
    return z.reshape(B, HP * WP, E)

@@ -1,0 +1,313 @@
+import math
+from contextlib import ExitStack
+
+import concourse.mybir as mybir
+from concourse.masks import make_identity
+
+F32 = mybir.dt.float32
+BF16 = mybir.dt.bfloat16
+U32 = mybir.dt.uint32
+U8 = mybir.dt.uint8
+FP8X4 = mybir.dt.float8_e4m3fn_x4
+ACT = mybir.ActivationFunctionType
+ALU = mybir.AluOpType
+
+P = 128
+PACK = 4
+E = 512
+F = 2048
+PASSES = F // (P * PACK)
+PLANES = PACK
+TOKENS = 2560
+TILES = TOKENS // P
+CHUNK = 512
+TILES_PER_CHUNK = CHUNK // P
+STEPS = (TOKENS // CHUNK) * PASSES
+WINDOW_ROWS = 8
+WINDOW_COLS = 5
+LN_EPS = 1e-5
+WORDS = E // 2
+
+FLOPS = 2 * TOKENS * E * F * 2
+
+RESIDUAL_LAG = 2
+MATMUL2_LAG = 4
+NORM_LAG = 5
+
+
+def tile_swintransformerblock_pb_kernel(tc, y, w1, b1, w2, b2, ln2_g, ln2_b, out):
+    nc = tc.nc
+
+    y_view = y.flatten_outer_dims().rearrange(
+        "(bw ww rx c) e -> ww bw rx (c e)", bw=WINDOW_ROWS, ww=WINDOW_COLS, rx=16, c=TILES_PER_CHUNK
+    )
+    out_view = out.flatten_outer_dims().rearrange(
+        "(bwr ww x c) e -> ww c x bwr e", bwr=64, ww=WINDOW_COLS, x=2, c=TILES_PER_CHUNK
+    )
+
+    with ExitStack() as ctx:
+        keep = ctx.enter_context(tc.tile_pool(name="keep", bufs=1))
+        group_pool = ctx.enter_context(tc.tile_pool(name="group", bufs=4))
+        plane_pool = ctx.enter_context(tc.tile_pool(name="plane", bufs=3))
+        hidden_pool = ctx.enter_context(tc.tile_pool(name="hidden", bufs=2))
+        resid_pool = ctx.enter_context(tc.tile_pool(name="resid", bufs=4))
+        norm_pool = ctx.enter_context(tc.tile_pool(name="norm", bufs=3))
+        stat_pool = ctx.enter_context(tc.tile_pool(name="stat", bufs=4))
+        psum_h = ctx.enter_context(tc.psum_pool(name="psum_h", bufs=4))
+        psum_f = ctx.enter_context(tc.psum_pool(name="psum_f", bufs=2))
+        psum_aux = ctx.enter_context(tc.psum_pool(name="psum_aux", bufs=2))
+
+        y_sb = keep.tile([P, TILES * E], BF16)
+        w1_sb = keep.tile([P, (F // P) * E], BF16)
+        w2_sb = keep.tile([P, (E // P) * F], BF16)
+        y_codes = keep.tile([P, TOKENS], U32, align_bytes=64)
+        y_scales = keep.tile([P, TOKENS], U8, align_bytes=64)
+        w1_codes = keep.tile([P, F], U32, align_bytes=64)
+        w1_scales = keep.tile([P, F], U8, align_bytes=64)
+        w2_codes = keep.tile([P, PASSES * E], U32, align_bytes=64)
+        w2_scales = keep.tile([P, PASSES * E], U8, align_bytes=64)
+        ident = keep.tile([P, P], F32)
+        ident_bf = keep.tile([P, P], BF16)
+        ones_bf = keep.tile([P, P], BF16)
+        b1_rows = keep.tile([P, 2 * P], BF16)
+        b1_pairs = keep.tile([P, F // P], BF16)
+        b1_col = keep.tile([P, F // P], F32)
+        b2_row = keep.tile([P, E], BF16)
+        gain_bf = keep.tile([P, E], BF16)
+        gain = keep.tile([P, E], F32)
+        shift_bf = keep.tile([P, E], BF16)
+        warm = keep.tile([P, 1], F32)
+        warm_out = keep.tile([P, 1], F32)
+        neg_half = keep.tile([P, 1], F32)
+
+        nc.vector.memset(warm[:], 0.0)
+        nc.vector.memset(b1_rows[:], 0.0)
+        nc.vector.memset(b2_row[:], 0.0)
+        nc.vector.memset(ones_bf[:], 1.0)
+        nc.vector.memset(neg_half[:], -0.5)
+        nc.scalar.activation(out=warm_out[:], in_=warm[:], func=ACT.Gelu)
+        make_identity(nc, ident[:])
+        make_identity(nc, ident_bf[:])
+
+        w1_view = w1.rearrange("(gu p e2) k -> p gu (e2 k)", gu=F // (2 * P), p=P, e2=2)
+        w1_slots = w1_sb[:].rearrange("p (gu n) -> p gu n", n=2 * E)
+        w2_view = w2.rearrange("(ec p) f -> p ec f", p=P)
+        w2_slots = w2_sb[:].rearrange("p (ec f) -> p ec f", f=F)
+
+        def load_w1(g):
+            nc.sync.dma_start(out=w1_slots[:, 2 * g : 2 * g + 2, :], in_=w1_view[:, 2 * g : 2 * g + 2, :])
+
+        def load_y(ww):
+            for bw in range(WINDOW_ROWS):
+                nc.sync.dma_start(
+                    out=y_sb[16 * bw : 16 * bw + 16, TILES_PER_CHUNK * E * ww : TILES_PER_CHUNK * E * (ww + 1)],
+                    in_=y_view[ww, bw],
+                )
+
+        load_w1(0)
+        nc.sync.dma_start(out=b1_rows[0:8, :], in_=b1.rearrange("(gu n) -> gu n", n=2 * P))
+        load_y(0)
+        for g in range(1, PASSES):
+            load_w1(g)
+        for ec in range(E // P):
+            nc.sync.dma_start(out=w2_slots[:, ec, :], in_=w2_view[:, ec, :])
+        for ww in range(1, WINDOW_COLS):
+            load_y(ww)
+        nc.gpsimd.dma_start(out=b2_row[0:1, :], in_=b2.rearrange("(o e) -> o e", o=1))
+        nc.gpsimd.dma_start(out=gain_bf[:], in_=ln2_g.partition_broadcast(P))
+        nc.gpsimd.dma_start(out=shift_bf[:], in_=ln2_b.partition_broadcast(P))
+
+        def transpose_group(words, base, block_step, pool, tag, vector_helps):
+            grouped = group_pool.tile([P, CHUNK * PACK], BF16, align_bytes=64, tag="grouped")
+            grouped_words = grouped[:].bitcast(F32)
+            for half in range(2):
+                bank = pool.tile([P, 2, 2 * P], F32, tag=tag)
+                for b in range(2):
+                    for u in range(2):
+                        first = base + block_step * (2 * half + b) + P * u
+                        nc.tensor.transpose(
+                            out=bank[:, u, P * b : P * (b + 1)], in_=words[:, first : first + P], identity=ident[:]
+                        )
+                pairs = grouped_words[:, CHUNK * half : CHUNK * (half + 1)].rearrange("p (c u) -> p c u", u=2)
+                if vector_helps and half == 1:
+                    nc.vector.tensor_copy(out=pairs, in_=bank[:].rearrange("p u c -> p c u"))
+                else:
+                    nc.scalar.copy(out=pairs, in_=bank[:].rearrange("p u c -> p c u"))
+            return grouped
+
+        def quantise(grouped, codes, scales):
+            nc.vector.quantize_mx(out=codes.bitcast(FP8X4), scales=scales, in_=grouped)
+
+        y_words = y_sb[:].bitcast(F32)
+        w1_words = w1_sb[:].bitcast(F32)
+        w2_words = w2_sb[:].bitcast(F32)
+
+        def transpose_w1(g):
+            return transpose_group(w1_words, PLANES * WORDS * g, WORDS, psum_aux, "aux", True)
+
+        def transpose_w2(g):
+            return transpose_group(w2_words, WORDS * g, F // 2, psum_f, "f", True)
+
+        def transpose_y(chunk):
+            return transpose_group(y_words, TILES_PER_CHUNK * WORDS * chunk, WORDS, psum_aux, "aux", False)
+
+        def columns(i):
+            return slice(CHUNK * i, CHUNK * (i + 1))
+
+        b1_bank = psum_aux.tile([P, 2, 2 * P], F32, tag="aux")
+        nc.tensor.transpose(out=b1_bank[:, 0, 0:P], in_=b1_rows[:].bitcast(F32), identity=ident[:])
+        nc.vector.tensor_copy(out=b1_pairs[:].bitcast(F32), in_=b1_bank[:, 0, 0 : F // (2 * P)])
+        nc.vector.tensor_copy(out=b1_col[:], in_=b1_pairs[:])
+
+        h_banks = {}
+        h_planes = {}
+        h_codes = {}
+        h_scales = {}
+        f_banks = {}
+        resid = {}
+        summed = {}
+        centred = {}
+        stats = {}
+
+        def matmul1_pass(step, k):
+            chunk, g = divmod(step, PASSES)
+            plane = slice(P * (PLANES * g + k), P * (PLANES * g + k + 1))
+            bank = psum_h.tile([P, CHUNK], F32, tag="h")
+            nc.tensor.matmul_mx(
+                out=bank[:],
+                lhsT=w1_codes[:, plane].bitcast(FP8X4),
+                lhsT_scale=w1_scales[:, plane],
+                rhs=y_codes[:, columns(chunk)].bitcast(FP8X4),
+                rhs_scale=y_scales[:, columns(chunk)],
+                start=True,
+                stop=True,
+            )
+            h_banks[(step, k)] = bank
+
+        def gelu(step):
+            g = step % PASSES
+            planes = plane_pool.tile([P, PLANES, CHUNK], BF16, tag="planes")
+            for k in range(PLANES):
+                j = PLANES * g + k
+                nc.scalar.activation(
+                    out=planes[:, k, :], in_=h_banks[(step, k)][:], func=ACT.Gelu, bias=b1_col[:, j : j + 1]
+                )
+            h_planes[step] = planes
+
+        def regroup(step):
+            grouped = group_pool.tile([P, CHUNK, PACK], BF16, align_bytes=64, tag="h_grouped")
+            nc.vector.tensor_copy(
+                out=grouped[:].rearrange("p (c i) t -> p c t i", i=4),
+                in_=h_planes[step][:].rearrange("p t (c i) -> p c t i", i=4),
+            )
+            return grouped
+
+        def quantise_hidden(step, grouped):
+            chunk, g = divmod(step, PASSES)
+            if g == 0:
+                h_codes[chunk] = hidden_pool.tile([P, PASSES, CHUNK], U32, align_bytes=64, tag="codes", name="codes")
+                h_scales[chunk] = hidden_pool.tile([P, PASSES, CHUNK], U8, align_bytes=64, tag="scales", name="scales")
+            quantise(grouped[:].rearrange("p r t -> p (r t)"), h_codes[chunk][:, g, :], h_scales[chunk][:, g, :])
+
+        def matmul2_pass(q, g):
+            chunk, t = divmod(q, TILES_PER_CHUNK)
+            if g == 0:
+                f_banks[q] = psum_f.tile([P, E], F32, tag="f", name="f_bank")
+            tokens = slice(P * t, P * (t + 1))
+            nc.tensor.matmul_mx(
+                out=f_banks[q][:],
+                lhsT=h_codes[chunk][:, g, tokens].bitcast(FP8X4),
+                lhsT_scale=h_scales[chunk][:, g, tokens],
+                rhs=w2_codes[:, columns(g)].bitcast(FP8X4),
+                rhs_scale=w2_scales[:, columns(g)],
+                start=(g == 0),
+                stop=(g == PASSES - 1),
+            )
+
+        def residual(q):
+            bank = psum_aux.tile([P, E], F32, tag="aux")
+            nc.tensor.matmul(out=bank[:], lhsT=ident_bf[:], rhs=y_sb[:, E * q : E * (q + 1)], start=True, stop=False)
+            nc.tensor.matmul(out=bank[:], lhsT=ones_bf[:], rhs=b2_row[:], start=False, stop=True)
+            resid[q] = resid_pool.tile([P, E], F32, tag="resid", name="resid")
+            nc.scalar.copy(out=resid[q][:], in_=bank[:])
+
+        def add_residual(q):
+            summed[q] = norm_pool.tile([P, E], F32, tag="summed", name="summed")
+            total = stat_pool.tile([P, 1], F32, tag="total")
+            nc.vector.scalar_tensor_tensor(
+                out=summed[q][:], in0=f_banks[q][:], scalar=1.0, in1=resid[q][:],
+                op0=ALU.mult, op1=ALU.add, accum_out=total[:],
+            )
+            return total
+
+        def centre(q, total):
+            neg_mean = stat_pool.tile([P, 1], F32, tag="neg_mean")
+            nc.vector.tensor_scalar_mul(out=neg_mean[:], in0=total[:], scalar1=-1.0 / E)
+            centred[q] = norm_pool.tile([P, E], F32, tag="centred", name="centred")
+            nc.vector.scalar_tensor_tensor(
+                out=centred[q][:], in0=summed[q][:], scalar=neg_mean[:], in1=gain[:], op0=ALU.add, op1=ALU.mult
+            )
+            stats[q] = neg_mean
+
+        def inverse_deviation(q):
+            squares = norm_pool.tile([P, E], BF16, tag="squares")
+            sum_squares = stat_pool.tile([P, 1], F32, tag="sum_squares")
+            nc.scalar.activation(
+                out=squares[:], in_=summed[q][:], func=ACT.Square, bias=stats[q][:], accum_out=sum_squares[:]
+            )
+            padded = stat_pool.tile([P, 1], F32, tag="padded")
+            nc.gpsimd.tensor_scalar(
+                out=padded[:], in0=sum_squares[:], scalar1=1.0, scalar2=E * LN_EPS, op0=ALU.mult, op1=ALU.add
+            )
+            inv_dev = stat_pool.tile([P, 1], F32, tag="inv_dev")
+            nc.gpsimd.tensor_tensor(out=inv_dev[:], in0=padded[:], in1=neg_half[:], op=ALU.pow)
+            return inv_dev
+
+        def scale_shift_store(q, inv_dev):
+            ww, c = divmod(q, TILES_PER_CHUNK)
+            z = norm_pool.tile([P, E], F32, tag="z")
+            nc.vector.scalar_tensor_tensor(
+                out=z[:], in0=centred[q][:], scalar=inv_dev[:], in1=shift_bf[:], op0=ALU.mult, op1=ALU.add
+            )
+            for x in range(2):
+                nc.sync.dma_start(out=out_view[ww, c, x], in_=z[x:P:2, :])
+
+        quantise(transpose_w1(0)[:], w1_codes[:, columns(0)], w1_scales[:, columns(0)])
+        quantise(transpose_y(0)[:], y_codes[:, columns(0)], y_scales[:, columns(0)])
+        for k in range(PLANES):
+            matmul1_pass(0, k)
+        quantise(transpose_w1(1)[:], w1_codes[:, columns(1)], w1_scales[:, columns(1)])
+        nc.vector.tensor_scalar_mul(out=gain[:], in0=gain_bf[:], scalar1=math.sqrt(E))
+
+        for i in range(STEPS + NORM_LAG):
+            q_resid, q_mm2, q_norm = i - RESIDUAL_LAG, i - MATMUL2_LAG, i - NORM_LAG
+            if i < STEPS:
+                gelu(i)
+            for k in range(PLANES):
+                if i + 1 < STEPS:
+                    matmul1_pass(i + 1, k)
+                if 0 <= q_mm2 < TILES:
+                    matmul2_pass(q_mm2, k)
+            if 0 <= q_resid < TILES:
+                residual(q_resid)
+            waiting = []
+            if i + 2 < PASSES:
+                waiting.append((transpose_w1(i + 2), w1_codes, w1_scales, i + 2))
+            if i < PASSES:
+                waiting.append((transpose_w2(i), w2_codes, w2_scales, i))
+            if i % PASSES == 1 and i // PASSES + 1 < TOKENS // CHUNK:
+                waiting.append((transpose_y(i // PASSES + 1), y_codes, y_scales, i // PASSES + 1))
+            if 0 <= q_norm < TILES:
+                inv_dev = inverse_deviation(q_norm)
+            if i < STEPS:
+                h_grouped = regroup(i)
+            if 0 <= q_mm2 < TILES:
+                total = add_residual(q_mm2)
+            for grouped, codes, scales, n in waiting:
+                quantise(grouped[:], codes[:, columns(n)], scales[:, columns(n)])
+            if i < STEPS:
+                quantise_hidden(i, h_grouped)
+            if 0 <= q_mm2 < TILES:
+                centre(q_mm2, total)
+            if 0 <= q_norm < TILES:
+                scale_shift_store(q_norm, inv_dev)

@@ -56,6 +56,7 @@ def tile_swintransformerblock_pb_kernel(tc, y, w1, b1, w2, b2, ln2_g, ln2_b, out
         psum_h = ctx.enter_context(tc.psum_pool(name="psum_h", bufs=4))
         psum_f = ctx.enter_context(tc.psum_pool(name="psum_f", bufs=2))
         psum_aux = ctx.enter_context(tc.psum_pool(name="psum_aux", bufs=2))
+        ctx.enter_context(tc.manual_schedule())
 
         y_sb = keep.tile([P, TILES * E], BF16)
         w1_sb = keep.tile([P, (F // P) * E], BF16)

@@ -1,4 +1,3 @@
-import math
 from contextlib import ExitStack
 
 import concourse.mybir as mybir
@@ -39,7 +38,7 @@ def tile_swintransformerblock_pb_kernel(tc, y, w1, b1, w2, b2, ln2_g, ln2_b, out
     nc = tc.nc
 
     y_view = y.flatten_outer_dims().rearrange(
-        "(bw ww rx c) e -> ww bw rx (c e)", bw=WINDOW_ROWS, ww=WINDOW_COLS, rx=16, c=TILES_PER_CHUNK
+        "(bw ww rx c) e -> bw rx ww (c e)", bw=WINDOW_ROWS, ww=WINDOW_COLS, rx=16, c=TILES_PER_CHUNK
     )
     out_view = out.flatten_outer_dims().rearrange(
         "(bwr ww x c) e -> ww c x bwr e", bwr=64, ww=WINDOW_COLS, x=2, c=TILES_PER_CHUNK
@@ -75,11 +74,13 @@ def tile_swintransformerblock_pb_kernel(tc, y, w1, b1, w2, b2, ln2_g, ln2_b, out
         b1_col = keep.tile([P, F // P], F32)
         b2_row = keep.tile([P, E], BF16)
         gain_bf = keep.tile([P, E], BF16)
-        gain = keep.tile([P, E], F32)
         shift_bf = keep.tile([P, E], BF16)
         warm = keep.tile([P, 1], F32)
         warm_out = keep.tile([P, 1], F32)
         neg_half = keep.tile([P, 1], F32)
+
+        def columns(i):
+            return slice(CHUNK * i, CHUNK * (i + 1))
 
         nc.vector.memset(warm[:], 0.0)
         nc.vector.memset(b1_rows[:], 0.0)
@@ -87,54 +88,56 @@ def tile_swintransformerblock_pb_kernel(tc, y, w1, b1, w2, b2, ln2_g, ln2_b, out
         nc.vector.memset(ones_bf[:], 1.0)
         nc.vector.memset(neg_half[:], -0.5)
         nc.scalar.activation(out=warm_out[:], in_=warm[:], func=ACT.Gelu)
+        nc.gpsimd.dma_start(out=b1_rows[0:8, :], in_=b1.rearrange("(gu n) -> gu n", n=2 * P))
         make_identity(nc, ident[:])
         make_identity(nc, ident_bf[:])
-
-        w1_view = w1.rearrange("(gu p e2) k -> p gu (e2 k)", gu=F // (2 * P), p=P, e2=2)
-        w1_slots = w1_sb[:].rearrange("p (gu n) -> p gu n", n=2 * E)
-        w2_view = w2.rearrange("(ec p) f -> p ec f", p=P)
-        w2_slots = w2_sb[:].rearrange("p (ec f) -> p ec f", f=F)
-
-        def load_w1(g):
-            nc.sync.dma_start(out=w1_slots[:, 2 * g : 2 * g + 2, :], in_=w1_view[:, 2 * g : 2 * g + 2, :])
-
-        def load_y(ww):
-            for bw in range(WINDOW_ROWS):
-                nc.sync.dma_start(
-                    out=y_sb[16 * bw : 16 * bw + 16, TILES_PER_CHUNK * E * ww : TILES_PER_CHUNK * E * (ww + 1)],
-                    in_=y_view[ww, bw],
-                )
-
-        load_w1(0)
-        nc.sync.dma_start(out=b1_rows[0:8, :], in_=b1.rearrange("(gu n) -> gu n", n=2 * P))
-        load_y(0)
-        for g in range(1, PASSES):
-            load_w1(g)
-        for ec in range(E // P):
-            nc.sync.dma_start(out=w2_slots[:, ec, :], in_=w2_view[:, ec, :])
-        for ww in range(1, WINDOW_COLS):
-            load_y(ww)
         nc.gpsimd.dma_start(out=b2_row[0:1, :], in_=b2.rearrange("(o e) -> o e", o=1))
         nc.gpsimd.dma_start(out=gain_bf[:], in_=ln2_g.partition_broadcast(P))
         nc.gpsimd.dma_start(out=shift_bf[:], in_=ln2_b.partition_broadcast(P))
 
-        def transpose_group(words, base, block_step, pool, tag, vector_helps):
-            grouped = group_pool.tile([P, CHUNK * PACK], BF16, align_bytes=64, tag="grouped")
-            grouped_words = grouped[:].bitcast(F32)
-            for half in range(2):
-                bank = pool.tile([P, 2, 2 * P], F32, tag=tag)
-                for b in range(2):
-                    for u in range(2):
-                        first = base + block_step * (2 * half + b) + P * u
-                        nc.tensor.transpose(
-                            out=bank[:, u, P * b : P * (b + 1)], in_=words[:, first : first + P], identity=ident[:]
-                        )
-                pairs = grouped_words[:, CHUNK * half : CHUNK * (half + 1)].rearrange("p (c u) -> p c u", u=2)
-                if vector_helps and half == 1:
-                    nc.vector.tensor_copy(out=pairs, in_=bank[:].rearrange("p u c -> p c u"))
-                else:
-                    nc.scalar.copy(out=pairs, in_=bank[:].rearrange("p u c -> p c u"))
-            return grouped
+        w1_view = w1.rearrange("(gu p e2) k -> p gu (e2 k)", gu=F // (2 * P), p=P, e2=2)
+        w1_slots = w1_sb[:].rearrange("p (gu n) -> p gu n", n=2 * E)
+        w2_view = w2.rearrange("(ec p) (g f) -> p g ec f", p=P, g=PASSES)
+        w2_slots = w2_sb[:].rearrange("p (g ec f) -> p g ec f", g=PASSES, f=P * PACK)
+        y_chunks = y_sb[:].rearrange("p (ww n) -> p ww n", ww=WINDOW_COLS)
+
+        def load_w1(g):
+            nc.sync.dma_start(out=w1_slots[:, 2 * g : 2 * g + 2, :], in_=w1_view[:, 2 * g : 2 * g + 2, :])
+
+        def load_w2(g):
+            nc.sync.dma_start(out=w2_slots[:, g], in_=w2_view[:, g])
+
+        def load_y(first_chunk, chunks):
+            for bw in range(WINDOW_ROWS):
+                nc.sync.dma_start(
+                    out=y_chunks[16 * bw : 16 * bw + 16, first_chunk : first_chunk + chunks, :],
+                    in_=y_view[bw, :, first_chunk : first_chunk + chunks, :],
+                )
+
+        load_w1(0)
+        load_y(0, 1)
+        for g in range(1, PASSES):
+            load_w1(g)
+        load_y(1, 1)
+        for g in range(PASSES):
+            load_w2(g)
+        load_y(2, WINDOW_COLS - 2)
+
+        def transpose_half(words, base, block_step, half, pool, tag):
+            bank = pool.tile([P, 2, 2 * P], F32, tag=tag)
+            for b in range(2):
+                for u in range(2):
+                    first = base + block_step * (2 * half + b) + P * u
+                    nc.tensor.transpose(
+                        out=bank[:, u, P * b : P * (b + 1)], in_=words[:, first : first + P], identity=ident[:]
+                    )
+            return bank
+
+        def new_group():
+            return group_pool.tile([P, CHUNK * PACK], BF16, align_bytes=64, tag="grouped", name="grouped")
+
+        def pairs_of(grouped, half):
+            return grouped[:].bitcast(F32)[:, CHUNK * half : CHUNK * (half + 1)].rearrange("p (c u) -> p c u", u=2)
 
         def quantise(grouped, codes, scales):
             nc.vector.quantize_mx(out=codes.bitcast(FP8X4), scales=scales, in_=grouped)
@@ -142,18 +145,6 @@ def tile_swintransformerblock_pb_kernel(tc, y, w1, b1, w2, b2, ln2_g, ln2_b, out
         y_words = y_sb[:].bitcast(F32)
         w1_words = w1_sb[:].bitcast(F32)
         w2_words = w2_sb[:].bitcast(F32)
-
-        def transpose_w1(g):
-            return transpose_group(w1_words, PLANES * WORDS * g, WORDS, psum_aux, "aux", True)
-
-        def transpose_w2(g):
-            return transpose_group(w2_words, WORDS * g, F // 2, psum_f, "f", True)
-
-        def transpose_y(chunk):
-            return transpose_group(y_words, TILES_PER_CHUNK * WORDS * chunk, WORDS, psum_aux, "aux", False)
-
-        def columns(i):
-            return slice(CHUNK * i, CHUNK * (i + 1))
 
         b1_bank = psum_aux.tile([P, 2, 2 * P], F32, tag="aux")
         nc.tensor.transpose(out=b1_bank[:, 0, 0:P], in_=b1_rows[:].bitcast(F32), identity=ident[:])
@@ -229,8 +220,7 @@ def tile_swintransformerblock_pb_kernel(tc, y, w1, b1, w2, b2, ln2_g, ln2_b, out
             bank = psum_aux.tile([P, E], F32, tag="aux")
             nc.tensor.matmul(out=bank[:], lhsT=ident_bf[:], rhs=y_sb[:, E * q : E * (q + 1)], start=True, stop=False)
             nc.tensor.matmul(out=bank[:], lhsT=ones_bf[:], rhs=b2_row[:], start=False, stop=True)
-            resid[q] = resid_pool.tile([P, E], F32, tag="resid", name="resid")
-            nc.scalar.copy(out=resid[q][:], in_=bank[:])
+            return bank
 
         def add_residual(q):
             summed[q] = norm_pool.tile([P, E], F32, tag="summed", name="summed")
@@ -246,7 +236,7 @@ def tile_swintransformerblock_pb_kernel(tc, y, w1, b1, w2, b2, ln2_g, ln2_b, out
             nc.vector.tensor_scalar_mul(out=neg_mean[:], in0=total[:], scalar1=-1.0 / E)
             centred[q] = norm_pool.tile([P, E], F32, tag="centred", name="centred")
             nc.vector.scalar_tensor_tensor(
-                out=centred[q][:], in0=summed[q][:], scalar=neg_mean[:], in1=gain[:], op0=ALU.add, op1=ALU.mult
+                out=centred[q][:], in0=summed[q][:], scalar=neg_mean[:], in1=gain_bf[:], op0=ALU.add, op1=ALU.mult
             )
             stats[q] = neg_mean
 
@@ -258,7 +248,7 @@ def tile_swintransformerblock_pb_kernel(tc, y, w1, b1, w2, b2, ln2_g, ln2_b, out
             )
             padded = stat_pool.tile([P, 1], F32, tag="padded")
             nc.gpsimd.tensor_scalar(
-                out=padded[:], in0=sum_squares[:], scalar1=1.0, scalar2=E * LN_EPS, op0=ALU.mult, op1=ALU.add
+                out=padded[:], in0=sum_squares[:], scalar1=1.0 / E, scalar2=LN_EPS, op0=ALU.mult, op1=ALU.add
             )
             inv_dev = stat_pool.tile([P, 1], F32, tag="inv_dev")
             nc.gpsimd.tensor_tensor(out=inv_dev[:], in0=padded[:], in1=neg_half[:], op=ALU.pow)
@@ -273,40 +263,60 @@ def tile_swintransformerblock_pb_kernel(tc, y, w1, b1, w2, b2, ln2_g, ln2_b, out
             for x in range(2):
                 nc.sync.dma_start(out=out_view[ww, c, x], in_=z[x:P:2, :])
 
-        quantise(transpose_w1(0)[:], w1_codes[:, columns(0)], w1_scales[:, columns(0)])
-        quantise(transpose_y(0)[:], y_codes[:, columns(0)], y_scales[:, columns(0)])
-        for k in range(PLANES):
-            matmul1_pass(0, k)
-        quantise(transpose_w1(1)[:], w1_codes[:, columns(1)], w1_scales[:, columns(1)])
-        nc.vector.tensor_scalar_mul(out=gain[:], in0=gain_bf[:], scalar1=math.sqrt(E))
+        weight_groups = [(w1_words, PLANES * WORDS * g, WORDS, w1_codes, w1_scales, g) for g in range(PASSES)]
+        weight_groups += [(w2_words, PLANES * WORDS * g, WORDS, w2_codes, w2_scales, g) for g in range(PASSES)]
+        first_round = MATMUL2_LAG - len(weight_groups)
 
-        for i in range(STEPS + NORM_LAG):
+        weight_banks = []
+        y_banks = []
+        resid_banks = []
+        y_grouped = {}
+        for i in range(first_round, STEPS + NORM_LAG):
             q_resid, q_mm2, q_norm = i - RESIDUAL_LAG, i - MATMUL2_LAG, i - NORM_LAG
-            if i < STEPS:
+            if 0 <= i < STEPS:
                 gelu(i)
+
+            for n, banks in weight_banks:
+                grouped = new_group()
+                nc.scalar.copy(out=pairs_of(grouped, 0), in_=banks[0][:].rearrange("p u c -> p c u"))
+                nc.vector.tensor_copy(out=pairs_of(grouped, 1), in_=banks[1][:].rearrange("p u c -> p c u"))
+                codes, scales, g = weight_groups[n][3:]
+                quantise(grouped[:], codes[:, columns(g)], scales[:, columns(g)])
+            for chunk, half, bank in y_banks:
+                if half == 0:
+                    y_grouped[chunk] = new_group()
+                nc.scalar.copy(out=pairs_of(y_grouped[chunk], half), in_=bank[:].rearrange("p u c -> p c u"))
+                if half == 1:
+                    quantise(y_grouped[chunk][:], y_codes[:, columns(chunk)], y_scales[:, columns(chunk)])
+            for q, bank in resid_banks:
+                resid[q] = resid_pool.tile([P, E], F32, tag="resid", name="resid")
+                nc.scalar.copy(out=resid[q][:], in_=bank[:])
+            if 0 <= q_norm < TILES:
+                inv_dev = inverse_deviation(q_norm)
+
             for k in range(PLANES):
-                if i + 1 < STEPS:
+                if 0 <= i + 1 < STEPS:
                     matmul1_pass(i + 1, k)
                 if 0 <= q_mm2 < TILES:
                     matmul2_pass(q_mm2, k)
+            weight_banks = []
+            n = i - first_round
+            if n < len(weight_groups):
+                words, base, block_step = weight_groups[n][:3]
+                weight_banks = [(n, [transpose_half(words, base, block_step, half, psum_f, "f") for half in range(2)])]
+            y_banks = []
+            chunk, half = divmod(i + PASSES, PASSES)
+            if chunk < TOKENS // CHUNK and half < 2:
+                y_banks = [(chunk, half, transpose_half(y_words, TILES_PER_CHUNK * WORDS * chunk, WORDS, half, psum_aux, "aux"))]
+            resid_banks = []
             if 0 <= q_resid < TILES:
-                residual(q_resid)
-            waiting = []
-            if i + 2 < PASSES:
-                waiting.append((transpose_w1(i + 2), w1_codes, w1_scales, i + 2))
-            if i < PASSES:
-                waiting.append((transpose_w2(i), w2_codes, w2_scales, i))
-            if i % PASSES == 1 and i // PASSES + 1 < TOKENS // CHUNK:
-                waiting.append((transpose_y(i // PASSES + 1), y_codes, y_scales, i // PASSES + 1))
-            if 0 <= q_norm < TILES:
-                inv_dev = inverse_deviation(q_norm)
-            if i < STEPS:
+                resid_banks = [(q_resid, residual(q_resid))]
+
+            if 0 <= i < STEPS:
                 h_grouped = regroup(i)
             if 0 <= q_mm2 < TILES:
                 total = add_residual(q_mm2)
-            for grouped, codes, scales, n in waiting:
-                quantise(grouped[:], codes[:, columns(n)], scales[:, columns(n)])
-            if i < STEPS:
+            if 0 <= i < STEPS:
                 quantise_hidden(i, h_grouped)
             if 0 <= q_mm2 < TILES:
                 centre(q_mm2, total)

@@ -31,7 +31,8 @@ FLOPS = 2 * TOKENS * E * F * 2
 
 RESIDUAL_LAG = 2
 MATMUL2_LAG = 4
-NORM_LAG = 5
+VARIANCE_LAG = 5
+SCALE_LAG = 6
 
 
 def tile_swintransformerblock_pb_kernel(tc, y, w1, b1, w2, b2, ln2_g, ln2_b, out):
@@ -51,6 +52,7 @@ def tile_swintransformerblock_pb_kernel(tc, y, w1, b1, w2, b2, ln2_g, ln2_b, out
         hidden_pool = ctx.enter_context(tc.tile_pool(name="hidden", bufs=2))
         resid_pool = ctx.enter_context(tc.tile_pool(name="resid", bufs=4))
         norm_pool = ctx.enter_context(tc.tile_pool(name="norm", bufs=3))
+        out_pool = ctx.enter_context(tc.tile_pool(name="out", bufs=4))
         stat_pool = ctx.enter_context(tc.tile_pool(name="stat", bufs=4))
         psum_h = ctx.enter_context(tc.psum_pool(name="psum_h", bufs=4))
         psum_f = ctx.enter_context(tc.psum_pool(name="psum_f", bufs=2))
@@ -78,6 +80,7 @@ def tile_swintransformerblock_pb_kernel(tc, y, w1, b1, w2, b2, ln2_g, ln2_b, out
         warm = keep.tile([P, 1], F32)
         warm_out = keep.tile([P, 1], F32)
         neg_half = keep.tile([P, 1], F32)
+        eps_col = keep.tile([P, 1], F32)
 
         def columns(i):
             return slice(CHUNK * i, CHUNK * (i + 1))
@@ -87,6 +90,7 @@ def tile_swintransformerblock_pb_kernel(tc, y, w1, b1, w2, b2, ln2_g, ln2_b, out
         nc.vector.memset(b2_row[:], 0.0)
         nc.vector.memset(ones_bf[:], 1.0)
         nc.vector.memset(neg_half[:], -0.5)
+        nc.vector.memset(eps_col[:], LN_EPS)
         nc.scalar.activation(out=warm_out[:], in_=warm[:], func=ACT.Gelu)
         nc.gpsimd.dma_start(out=b1_rows[0:8, :], in_=b1.rearrange("(gu n) -> gu n", n=2 * P))
         make_identity(nc, ident[:])
@@ -160,6 +164,7 @@ def tile_swintransformerblock_pb_kernel(tc, y, w1, b1, w2, b2, ln2_g, ln2_b, out
         summed = {}
         centred = {}
         stats = {}
+        inv_dev = {}
 
         def matmul1_pass(step, k):
             chunk, g = divmod(step, PASSES)
@@ -247,18 +252,15 @@ def tile_swintransformerblock_pb_kernel(tc, y, w1, b1, w2, b2, ln2_g, ln2_b, out
                 out=squares[:], in_=summed[q][:], func=ACT.Square, bias=stats[q][:], accum_out=sum_squares[:]
             )
             padded = stat_pool.tile([P, 1], F32, tag="padded")
-            nc.gpsimd.tensor_scalar(
-                out=padded[:], in0=sum_squares[:], scalar1=1.0 / E, scalar2=LN_EPS, op0=ALU.mult, op1=ALU.add
-            )
-            inv_dev = stat_pool.tile([P, 1], F32, tag="inv_dev")
-            nc.gpsimd.tensor_tensor(out=inv_dev[:], in0=padded[:], in1=neg_half[:], op=ALU.pow)
-            return inv_dev
+            nc.scalar.activation(out=padded[:], in_=sum_squares[:], func=ACT.Identity, bias=eps_col[:], scale=1.0 / E)
+            inv_dev[q] = stat_pool.tile([P, 1], F32, tag="inv_dev", name="inv_dev")
+            nc.gpsimd.tensor_tensor(out=inv_dev[q][:], in0=padded[:], in1=neg_half[:], op=ALU.pow)
 
-        def scale_shift_store(q, inv_dev):
+        def scale_shift_store(q):
             ww, c = divmod(q, TILES_PER_CHUNK)
-            z = norm_pool.tile([P, E], F32, tag="z")
+            z = out_pool.tile([P, E], F32, tag="z")
             nc.vector.scalar_tensor_tensor(
-                out=z[:], in0=centred[q][:], scalar=inv_dev[:], in1=shift_bf[:], op0=ALU.mult, op1=ALU.add
+                out=z[:], in0=centred[q][:], scalar=inv_dev[q][:], in1=shift_bf[:], op0=ALU.mult, op1=ALU.add
             )
             for x in range(2):
                 nc.sync.dma_start(out=out_view[ww, c, x], in_=z[x:P:2, :])
@@ -271,8 +273,8 @@ def tile_swintransformerblock_pb_kernel(tc, y, w1, b1, w2, b2, ln2_g, ln2_b, out
         y_banks = []
         resid_banks = []
         y_grouped = {}
-        for i in range(first_round, STEPS + NORM_LAG):
-            q_resid, q_mm2, q_norm = i - RESIDUAL_LAG, i - MATMUL2_LAG, i - NORM_LAG
+        for i in range(first_round, STEPS + SCALE_LAG):
+            q_resid, q_mm2, q_var, q_out = i - RESIDUAL_LAG, i - MATMUL2_LAG, i - VARIANCE_LAG, i - SCALE_LAG
             if 0 <= i < STEPS:
                 gelu(i)
 
@@ -291,8 +293,8 @@ def tile_swintransformerblock_pb_kernel(tc, y, w1, b1, w2, b2, ln2_g, ln2_b, out
             for q, bank in resid_banks:
                 resid[q] = resid_pool.tile([P, E], F32, tag="resid", name="resid")
                 nc.scalar.copy(out=resid[q][:], in_=bank[:])
-            if 0 <= q_norm < TILES:
-                inv_dev = inverse_deviation(q_norm)
+            if 0 <= q_var < TILES:
+                inverse_deviation(q_var)
 
             for k in range(PLANES):
                 if 0 <= i + 1 < STEPS:
@@ -320,5 +322,5 @@ def tile_swintransformerblock_pb_kernel(tc, y, w1, b1, w2, b2, ln2_g, ln2_b, out
                 quantise_hidden(i, h_grouped)
             if 0 <= q_mm2 < TILES:
                 centre(q_mm2, total)
-            if 0 <= q_norm < TILES:
-                scale_shift_store(q_norm, inv_dev)
+            if 0 <= q_out < TILES:
+                scale_shift_store(q_out)

@@ -60,6 +60,7 @@ def tile_swintransformerblock_pb_kernel(tc, y, w1, b1, w2, b2, ln2_g, ln2_b, out
         ctx.enter_context(tc.manual_schedule())
 
         y_sb = keep.tile([P, TILES * E], BF16)
+        y_win = keep.tile([P, TILES * E], BF16)
         w1_sb = keep.tile([P, (F // P) * E], BF16)
         w2_sb = keep.tile([P, (E // P) * F], BF16)
         y_codes = keep.tile([P, TOKENS], U32, align_bytes=64)
@@ -92,18 +93,16 @@ def tile_swintransformerblock_pb_kernel(tc, y, w1, b1, w2, b2, ln2_g, ln2_b, out
         nc.vector.memset(neg_half[:], -0.5)
         nc.vector.memset(eps_col[:], LN_EPS)
         nc.scalar.activation(out=warm_out[:], in_=warm[:], func=ACT.Gelu)
-        nc.gpsimd.dma_start(out=b1_rows[0:8, :], in_=b1.rearrange("(gu n) -> gu n", n=2 * P))
-        make_identity(nc, ident[:])
-        make_identity(nc, ident_bf[:])
-        nc.gpsimd.dma_start(out=b2_row[0:1, :], in_=b2.rearrange("(o e) -> o e", o=1))
-        nc.gpsimd.dma_start(out=gain_bf[:], in_=ln2_g.partition_broadcast(P))
-        nc.gpsimd.dma_start(out=shift_bf[:], in_=ln2_b.partition_broadcast(P))
 
         w1_view = w1.rearrange("(gu p e2) k -> p gu (e2 k)", gu=F // (2 * P), p=P, e2=2)
         w1_slots = w1_sb[:].rearrange("p (gu n) -> p gu n", n=2 * E)
         w2_view = w2.rearrange("(ec p) (g f) -> p g ec f", p=P, g=PASSES)
         w2_slots = w2_sb[:].rearrange("p (g ec f) -> p g ec f", g=PASSES, f=P * PACK)
         y_chunks = y_sb[:].rearrange("p (ww n) -> p ww n", ww=WINDOW_COLS)
+        y_win_view = y.flatten_outer_dims().rearrange(
+            "(bwp w ww n) e -> w ww n bwp e", bwp=WINDOW_ROWS // 2, w=2, ww=WINDOW_COLS
+        )
+        y_win_chunks = y_win[:].rearrange("p (ww bwp e) -> p ww bwp e", ww=WINDOW_COLS, e=E)
 
         def load_w1(g):
             nc.sync.dma_start(out=w1_slots[:, 2 * g : 2 * g + 2, :], in_=w1_view[:, 2 * g : 2 * g + 2, :])
@@ -118,14 +117,27 @@ def tile_swintransformerblock_pb_kernel(tc, y, w1, b1, w2, b2, ln2_g, ln2_b, out
                     in_=y_view[bw, :, first_chunk : first_chunk + chunks, :],
                 )
 
-        load_w1(0)
-        load_y(0, 1)
-        for g in range(1, PASSES):
+        make_identity(nc, ident[:])
+        nc.gpsimd.dma_start(out=b1_rows[0:8, :], in_=b1.rearrange("(gu n) -> gu n", n=2 * P))
+        make_identity(nc, ident_bf[:])
+        nc.gpsimd.dma_start(out=b2_row[0:1, :], in_=b2.rearrange("(o e) -> o e", o=1))
+        nc.gpsimd.dma_start(out=gain_bf[:], in_=ln2_g.partition_broadcast(P))
+        nc.gpsimd.dma_start(out=shift_bf[:], in_=ln2_b.partition_broadcast(P))
+        def load_y_win(ww):
+            for w in range(2):
+                nc.sync.dma_start(out=y_win_chunks[64 * w : 64 * (w + 1), ww], in_=y_win_view[w, ww])
+
+        load_y_win(0)
+        for g in range(PASSES):
             load_w1(g)
-        load_y(1, 1)
+        load_y_win(1)
         for g in range(PASSES):
             load_w2(g)
+        load_y(0, 2)
+        load_y_win(2)
         load_y(2, WINDOW_COLS - 2)
+        load_y_win(3)
+        load_y_win(4)
 
         def transpose_half(words, base, block_step, half, pool, tag):
             bank = pool.tile([P, 2, 2 * P], F32, tag=tag)
@@ -146,14 +158,15 @@ def tile_swintransformerblock_pb_kernel(tc, y, w1, b1, w2, b2, ln2_g, ln2_b, out
         def quantise(grouped, codes, scales):
             nc.vector.quantize_mx(out=codes.bitcast(FP8X4), scales=scales, in_=grouped)
 
-        y_words = y_sb[:].bitcast(F32)
+        y_words = y_win[:].bitcast(F32)
         w1_words = w1_sb[:].bitcast(F32)
         w2_words = w2_sb[:].bitcast(F32)
 
-        b1_bank = psum_aux.tile([P, 2, 2 * P], F32, tag="aux")
-        nc.tensor.transpose(out=b1_bank[:, 0, 0:P], in_=b1_rows[:].bitcast(F32), identity=ident[:])
-        nc.vector.tensor_copy(out=b1_pairs[:].bitcast(F32), in_=b1_bank[:, 0, 0 : F // (2 * P)])
-        nc.vector.tensor_copy(out=b1_col[:], in_=b1_pairs[:])
+        def spread_b1():
+            b1_bank = psum_aux.tile([P, 2, 2 * P], F32, tag="aux")
+            nc.tensor.transpose(out=b1_bank[:, 0, 0:P], in_=b1_rows[:].bitcast(F32), identity=ident[:])
+            nc.vector.tensor_copy(out=b1_pairs[:].bitcast(F32), in_=b1_bank[:, 0, 0 : F // (2 * P)])
+            nc.vector.tensor_copy(out=b1_col[:], in_=b1_pairs[:])
 
         h_banks = {}
         h_planes = {}
@@ -163,7 +176,9 @@ def tile_swintransformerblock_pb_kernel(tc, y, w1, b1, w2, b2, ln2_g, ln2_b, out
         resid = {}
         summed = {}
         centred = {}
-        stats = {}
+        neg_mean = {}
+        totals = {}
+        sums_of_squares = {}
         inv_dev = {}
 
         def matmul1_pass(step, k):
@@ -229,30 +244,34 @@ def tile_swintransformerblock_pb_kernel(tc, y, w1, b1, w2, b2, ln2_g, ln2_b, out
 
         def add_residual(q):
             summed[q] = norm_pool.tile([P, E], F32, tag="summed", name="summed")
-            total = stat_pool.tile([P, 1], F32, tag="total")
+            totals[q] = stat_pool.tile([P, 1], F32, tag="total", name="total")
             nc.vector.scalar_tensor_tensor(
                 out=summed[q][:], in0=f_banks[q][:], scalar=1.0, in1=resid[q][:],
-                op0=ALU.mult, op1=ALU.add, accum_out=total[:],
+                op0=ALU.mult, op1=ALU.add, accum_out=totals[q][:],
             )
-            return total
 
-        def centre(q, total):
-            neg_mean = stat_pool.tile([P, 1], F32, tag="neg_mean")
-            nc.vector.tensor_scalar_mul(out=neg_mean[:], in0=total[:], scalar1=-1.0 / E)
+        def negative_mean(q):
+            neg_mean[q] = stat_pool.tile([P, 1], F32, tag="neg_mean", name="neg_mean")
+            nc.vector.tensor_scalar_mul(out=neg_mean[q][:], in0=totals[q][:], scalar1=-1.0 / E)
+
+        def centre(q):
             centred[q] = norm_pool.tile([P, E], F32, tag="centred", name="centred")
             nc.vector.scalar_tensor_tensor(
-                out=centred[q][:], in0=summed[q][:], scalar=neg_mean[:], in1=gain_bf[:], op0=ALU.add, op1=ALU.mult
+                out=centred[q][:], in0=summed[q][:], scalar=neg_mean[q][:], in1=gain_bf[:], op0=ALU.add, op1=ALU.mult
             )
-            stats[q] = neg_mean
+
+        def sum_of_squares(q):
+            squares = norm_pool.tile([P, E], BF16, tag="squares")
+            sums_of_squares[q] = stat_pool.tile([P, 1], F32, tag="sum_squares", name="sum_squares")
+            nc.scalar.activation(
+                out=squares[:], in_=summed[q][:], func=ACT.Square, bias=neg_mean[q][:], accum_out=sums_of_squares[q][:]
+            )
 
         def inverse_deviation(q):
-            squares = norm_pool.tile([P, E], BF16, tag="squares")
-            sum_squares = stat_pool.tile([P, 1], F32, tag="sum_squares")
-            nc.scalar.activation(
-                out=squares[:], in_=summed[q][:], func=ACT.Square, bias=stats[q][:], accum_out=sum_squares[:]
-            )
             padded = stat_pool.tile([P, 1], F32, tag="padded")
-            nc.scalar.activation(out=padded[:], in_=sum_squares[:], func=ACT.Identity, bias=eps_col[:], scale=1.0 / E)
+            nc.scalar.activation(
+                out=padded[:], in_=sums_of_squares[q][:], func=ACT.Identity, bias=eps_col[:], scale=1.0 / E
+            )
             inv_dev[q] = stat_pool.tile([P, 1], F32, tag="inv_dev", name="inv_dev")
             nc.gpsimd.tensor_tensor(out=inv_dev[q][:], in0=padded[:], in1=neg_half[:], op=ALU.pow)
 
@@ -278,23 +297,36 @@ def tile_swintransformerblock_pb_kernel(tc, y, w1, b1, w2, b2, ln2_g, ln2_b, out
             if 0 <= i < STEPS:
                 gelu(i)
 
+            complete = []
             for n, banks in weight_banks:
                 grouped = new_group()
                 nc.scalar.copy(out=pairs_of(grouped, 0), in_=banks[0][:].rearrange("p u c -> p c u"))
                 nc.vector.tensor_copy(out=pairs_of(grouped, 1), in_=banks[1][:].rearrange("p u c -> p c u"))
                 codes, scales, g = weight_groups[n][3:]
-                quantise(grouped[:], codes[:, columns(g)], scales[:, columns(g)])
+                complete.append((grouped, codes, scales, g))
             for chunk, half, bank in y_banks:
                 if half == 0:
                     y_grouped[chunk] = new_group()
-                nc.scalar.copy(out=pairs_of(y_grouped[chunk], half), in_=bank[:].rearrange("p u c -> p c u"))
+                nc.scalar.copy(
+                    out=y_grouped[chunk][:]
+                    .bitcast(F32)
+                    .rearrange("p (c m u) -> p c m u", c=TILES_PER_CHUNK, u=2)[:, :, 64 * half : 64 * (half + 1), :],
+                    in_=bank[:].rearrange("p u (m c) -> p c m u", c=TILES_PER_CHUNK),
+                )
                 if half == 1:
-                    quantise(y_grouped[chunk][:], y_codes[:, columns(chunk)], y_scales[:, columns(chunk)])
+                    complete.append((y_grouped[chunk], y_codes, y_scales, chunk))
+            if 0 <= q_var < TILES:
+                sum_of_squares(q_var)
             for q, bank in resid_banks:
                 resid[q] = resid_pool.tile([P, E], F32, tag="resid", name="resid")
                 nc.scalar.copy(out=resid[q][:], in_=bank[:])
             if 0 <= q_var < TILES:
                 inverse_deviation(q_var)
+
+            if 0 <= i < STEPS:
+                h_grouped = regroup(i)
+            for grouped, codes, scales, g in complete:
+                quantise(grouped[:], codes[:, columns(g)], scales[:, columns(g)])
 
             for k in range(PLANES):
                 if 0 <= i + 1 < STEPS:
@@ -313,14 +345,16 @@ def tile_swintransformerblock_pb_kernel(tc, y, w1, b1, w2, b2, ln2_g, ln2_b, out
             resid_banks = []
             if 0 <= q_resid < TILES:
                 resid_banks = [(q_resid, residual(q_resid))]
+            if i == first_round:
+                spread_b1()
 
-            if 0 <= i < STEPS:
-                h_grouped = regroup(i)
             if 0 <= q_mm2 < TILES:
-                total = add_residual(q_mm2)
+                add_residual(q_mm2)
             if 0 <= i < STEPS:
                 quantise_hidden(i, h_grouped)
             if 0 <= q_mm2 < TILES:
-                centre(q_mm2, total)
+                negative_mean(q_mm2)
             if 0 <= q_out < TILES:
                 scale_shift_store(q_out)
+            if 0 <= q_mm2 < TILES:
+                centre(q_mm2)

@@ -29,8 +29,14 @@ WORDS = E // 2
 
 FLOPS = 2 * TOKENS * E * F * 2
 
+WORD_HALF = 2 * P
+
+LAST_CHUNK = TILES - TILES_PER_CHUNK
+HALF = CHUNK // 2
+
 RESIDUAL_LAG = 2
-MATMUL2_LAG = 4
+RESIDUAL_COPY_LAG = 3
+ADD_LAG = 4
 VARIANCE_LAG = 5
 SCALE_LAG = 6
 
@@ -50,8 +56,10 @@ def tile_swintransformerblock_pb_kernel(tc, y, w1, b1, w2, b2, ln2_g, ln2_b, out
         group_pool = ctx.enter_context(tc.tile_pool(name="group", bufs=4))
         plane_pool = ctx.enter_context(tc.tile_pool(name="plane", bufs=3))
         hidden_pool = ctx.enter_context(tc.tile_pool(name="hidden", bufs=2))
-        resid_pool = ctx.enter_context(tc.tile_pool(name="resid", bufs=4))
-        norm_pool = ctx.enter_context(tc.tile_pool(name="norm", bufs=3))
+        resid_pool = ctx.enter_context(tc.tile_pool(name="resid", bufs=3))
+        summed_pool = ctx.enter_context(tc.tile_pool(name="summed", bufs=3))
+        norm_pool = ctx.enter_context(tc.tile_pool(name="norm", bufs=2))
+        centred_pool = ctx.enter_context(tc.tile_pool(name="centred", bufs=5))
         out_pool = ctx.enter_context(tc.tile_pool(name="out", bufs=4))
         stat_pool = ctx.enter_context(tc.tile_pool(name="stat", bufs=4))
         psum_h = ctx.enter_context(tc.psum_pool(name="psum_h", bufs=4))
@@ -71,17 +79,17 @@ def tile_swintransformerblock_pb_kernel(tc, y, w1, b1, w2, b2, ln2_g, ln2_b, out
         w2_scales = keep.tile([P, PASSES * E], U8, align_bytes=64)
         ident = keep.tile([P, P], F32)
         ident_bf = keep.tile([P, P], BF16)
-        ones_bf = keep.tile([P, P], BF16)
         b1_rows = keep.tile([P, 2 * P], BF16)
         b1_pairs = keep.tile([P, F // P], BF16)
         b1_col = keep.tile([P, F // P], F32)
+        ones_bf = keep.tile([P, P], BF16)
         b2_row = keep.tile([P, E], BF16)
+        eps_col = keep.tile([P, 1], F32)
         gain_bf = keep.tile([P, E], BF16)
         shift_bf = keep.tile([P, E], BF16)
         warm = keep.tile([P, 1], F32)
         warm_out = keep.tile([P, 1], F32)
         neg_half = keep.tile([P, 1], F32)
-        eps_col = keep.tile([P, 1], F32)
 
         def columns(i):
             return slice(CHUNK * i, CHUNK * (i + 1))
@@ -90,8 +98,8 @@ def tile_swintransformerblock_pb_kernel(tc, y, w1, b1, w2, b2, ln2_g, ln2_b, out
         nc.vector.memset(b1_rows[:], 0.0)
         nc.vector.memset(b2_row[:], 0.0)
         nc.vector.memset(ones_bf[:], 1.0)
-        nc.vector.memset(neg_half[:], -0.5)
         nc.vector.memset(eps_col[:], LN_EPS)
+        nc.vector.memset(neg_half[:], -0.5)
         nc.scalar.activation(out=warm_out[:], in_=warm[:], func=ACT.Gelu)
 
         w1_view = w1.rearrange("(gu p e2) k -> p gu (e2 k)", gu=F // (2 * P), p=P, e2=2)
@@ -117,15 +125,16 @@ def tile_swintransformerblock_pb_kernel(tc, y, w1, b1, w2, b2, ln2_g, ln2_b, out
                     in_=y_view[bw, :, first_chunk : first_chunk + chunks, :],
                 )
 
+        def load_y_win(ww):
+            for w in range(2):
+                nc.sync.dma_start(out=y_win_chunks[64 * w : 64 * (w + 1), ww], in_=y_win_view[w, ww])
+
+        nc.sync.dma_start(out=b1_rows[0:8, :], in_=b1.rearrange("(gu n) -> gu n", n=2 * P))
         make_identity(nc, ident[:])
-        nc.gpsimd.dma_start(out=b1_rows[0:8, :], in_=b1.rearrange("(gu n) -> gu n", n=2 * P))
         make_identity(nc, ident_bf[:])
         nc.gpsimd.dma_start(out=b2_row[0:1, :], in_=b2.rearrange("(o e) -> o e", o=1))
         nc.gpsimd.dma_start(out=gain_bf[:], in_=ln2_g.partition_broadcast(P))
         nc.gpsimd.dma_start(out=shift_bf[:], in_=ln2_b.partition_broadcast(P))
-        def load_y_win(ww):
-            for w in range(2):
-                nc.sync.dma_start(out=y_win_chunks[64 * w : 64 * (w + 1), ww], in_=y_win_view[w, ww])
 
         load_y_win(0)
         for g in range(PASSES):
@@ -139,11 +148,11 @@ def tile_swintransformerblock_pb_kernel(tc, y, w1, b1, w2, b2, ln2_g, ln2_b, out
         load_y_win(3)
         load_y_win(4)
 
-        def transpose_half(words, base, block_step, half, pool, tag):
-            bank = pool.tile([P, 2, 2 * P], F32, tag=tag)
+        def transpose_half(words, base, half, pool, tag):
+            bank = pool.tile([P, 2, 2 * P], F32, tag=tag, name="words_bank")
             for b in range(2):
                 for u in range(2):
-                    first = base + block_step * (2 * half + b) + P * u
+                    first = base + WORDS * (2 * half + b) + P * u
                     nc.tensor.transpose(
                         out=bank[:, u, P * b : P * (b + 1)], in_=words[:, first : first + P], identity=ident[:]
                     )
@@ -152,9 +161,6 @@ def tile_swintransformerblock_pb_kernel(tc, y, w1, b1, w2, b2, ln2_g, ln2_b, out
         def new_group():
             return group_pool.tile([P, CHUNK * PACK], BF16, align_bytes=64, tag="grouped", name="grouped")
 
-        def pairs_of(grouped, half):
-            return grouped[:].bitcast(F32)[:, CHUNK * half : CHUNK * (half + 1)].rearrange("p (c u) -> p c u", u=2)
-
         def quantise(grouped, codes, scales):
             nc.vector.quantize_mx(out=codes.bitcast(FP8X4), scales=scales, in_=grouped)
 
@@ -162,69 +168,134 @@ def tile_swintransformerblock_pb_kernel(tc, y, w1, b1, w2, b2, ln2_g, ln2_b, out
         w1_words = w1_sb[:].bitcast(F32)
         w2_words = w2_sb[:].bitcast(F32)
 
+        weights = [(w1_words, w1_codes, w1_scales, g) for g in range(PASSES)]
+        weights += [(w2_words, w2_codes, w2_scales, g) for g in range(PASSES)]
+        weight_banks = {}
+        weight_grouped = {}
+
+        def weight_transposes(n, places):
+            words, codes, scales, g = weights[n]
+            weight_banks[n] = [
+                transpose_half(words, PLANES * WORDS * g, half, *places[half]) for half in range(2)
+            ]
+
+        def weight_copy(n, half, engine_copy):
+            if n not in weight_grouped:
+                weight_grouped[n] = new_group()
+            pairs = weight_grouped[n][:].bitcast(F32)[:, CHUNK * half : CHUNK * (half + 1)].rearrange(
+                "p (c u) -> p c u", u=2
+            )
+            engine_copy(out=pairs, in_=weight_banks[n][half][:].rearrange("p u c -> p c u"))
+
+        def weight_quantise(n):
+            words, codes, scales, g = weights[n]
+            quantise(weight_grouped[n][:], codes[:, columns(g)], scales[:, columns(g)])
+
+        y_banks = {}
+        y_grouped = {}
+
+        def y_transposes(chunk, half, place):
+            y_banks[(chunk, half)] = transpose_half(y_words, TILES_PER_CHUNK * WORDS * chunk, half, *place)
+
+        def y_copy(chunk, half, engine_copy):
+            if chunk not in y_grouped:
+                y_grouped[chunk] = new_group()
+            engine_copy(
+                out=y_grouped[chunk][:]
+                .bitcast(F32)
+                .rearrange("p (c m u) -> p c m u", c=TILES_PER_CHUNK, u=2)[:, :, 64 * half : 64 * (half + 1), :],
+                in_=y_banks[(chunk, half)][:].rearrange("p u (m c) -> p c m u", c=TILES_PER_CHUNK),
+            )
+
+        def y_quantise(chunk):
+            quantise(y_grouped[chunk][:], y_codes[:, columns(chunk)], y_scales[:, columns(chunk)])
+
         def spread_b1():
-            b1_bank = psum_aux.tile([P, 2, 2 * P], F32, tag="aux")
-            nc.tensor.transpose(out=b1_bank[:, 0, 0:P], in_=b1_rows[:].bitcast(F32), identity=ident[:])
-            nc.vector.tensor_copy(out=b1_pairs[:].bitcast(F32), in_=b1_bank[:, 0, 0 : F // (2 * P)])
+            bank = psum_h.tile([P, CHUNK], F32, tag="h", name="b1_bank")
+            nc.tensor.transpose(out=bank[:, 0:P], in_=b1_rows[:].bitcast(F32), identity=ident[:])
+            nc.vector.tensor_copy(out=b1_pairs[:].bitcast(F32), in_=bank[:, 0 : F // (2 * P)])
             nc.vector.tensor_copy(out=b1_col[:], in_=b1_pairs[:])
 
         h_banks = {}
         h_planes = {}
+        h_grouped = {}
         h_codes = {}
         h_scales = {}
         f_banks = {}
+        resid_banks = {}
         resid = {}
         summed = {}
-        centred = {}
-        neg_mean = {}
         totals = {}
+        neg_mean = {}
+        centred = {}
         sums_of_squares = {}
         inv_dev = {}
 
-        def matmul1_pass(step, k):
-            chunk, g = divmod(step, PASSES)
-            plane = slice(P * (PLANES * g + k), P * (PLANES * g + k + 1))
-            bank = psum_h.tile([P, CHUNK], F32, tag="h")
-            nc.tensor.matmul_mx(
-                out=bank[:],
-                lhsT=w1_codes[:, plane].bitcast(FP8X4),
-                lhsT_scale=w1_scales[:, plane],
-                rhs=y_codes[:, columns(chunk)].bitcast(FP8X4),
-                rhs_scale=y_scales[:, columns(chunk)],
-                start=True,
-                stop=True,
-            )
-            h_banks[(step, k)] = bank
+        def pieces(step):
+            return [(0, HALF), (HALF, HALF)] if step == STEPS - 1 else [(0, CHUNK)]
 
-        def gelu(step):
-            g = step % PASSES
-            planes = plane_pool.tile([P, PLANES, CHUNK], BF16, tag="planes")
-            for k in range(PLANES):
-                j = PLANES * g + k
-                nc.scalar.activation(
-                    out=planes[:, k, :], in_=h_banks[(step, k)][:], func=ACT.Gelu, bias=b1_col[:, j : j + 1]
+        def step_passes(step, j):
+            passes = [(first, w, k) for first, w in pieces(step) for k in range(PLANES)]
+            per_bank = len(passes) // PLANES
+            return passes[per_bank * j : per_bank * (j + 1)]
+
+        def matmul1_bank(step, j):
+            chunk, g = divmod(step, PASSES)
+            bank = psum_h.tile([P, CHUNK], F32, tag="h", name="h_bank")
+            for n, (first, w, k) in enumerate(step_passes(step, j)):
+                plane = slice(P * (PLANES * g + k), P * (PLANES * g + k + 1))
+                tokens = slice(CHUNK * chunk + first, CHUNK * chunk + first + w)
+                nc.tensor.matmul_mx(
+                    out=bank[:, w * n : w * (n + 1)],
+                    lhsT=w1_codes[:, plane].bitcast(FP8X4),
+                    lhsT_scale=w1_scales[:, plane],
+                    rhs=y_codes[:, tokens].bitcast(FP8X4),
+                    rhs_scale=y_scales[:, tokens],
+                    start=True,
+                    stop=True,
                 )
-            h_planes[step] = planes
+            h_banks[(step, j)] = bank
 
-        def regroup(step):
-            grouped = group_pool.tile([P, CHUNK, PACK], BF16, align_bytes=64, tag="h_grouped")
-            nc.vector.tensor_copy(
-                out=grouped[:].rearrange("p (c i) t -> p c t i", i=4),
-                in_=h_planes[step][:].rearrange("p t (c i) -> p c t i", i=4),
-            )
-            return grouped
-
-        def quantise_hidden(step, grouped):
+        def gelu_bank(step, j):
             chunk, g = divmod(step, PASSES)
-            if g == 0:
+            if j == 0:
+                h_planes[step] = plane_pool.tile([P, PLANES, CHUNK], BF16, tag="planes", name="planes")
+                h_grouped[step] = group_pool.tile(
+                    [P, CHUNK, PACK], BF16, align_bytes=64, tag="h_grouped", name="h_grouped"
+                )
+            for n, (first, w, k) in enumerate(step_passes(step, j)):
+                plane = PLANES * g + k
+                nc.scalar.activation(
+                    out=h_planes[step][:, k, first : first + w],
+                    in_=h_banks[(step, j)][:, w * n : w * (n + 1)],
+                    func=ACT.Gelu,
+                    bias=b1_col[:, plane : plane + 1],
+                )
+
+        def regroup(step, piece):
+            first, w = pieces(step)[piece]
+            nc.vector.tensor_copy(
+                out=h_grouped[step][:, first : first + w, :].rearrange("p (c i) t -> p c t i", i=4),
+                in_=h_planes[step][:, :, first : first + w].rearrange("p t (c i) -> p c t i", i=4),
+            )
+
+        def quantise_hidden(step, piece):
+            chunk, g = divmod(step, PASSES)
+            first, w = pieces(step)[piece]
+            if g == 0 and piece == 0:
                 h_codes[chunk] = hidden_pool.tile([P, PASSES, CHUNK], U32, align_bytes=64, tag="codes", name="codes")
                 h_scales[chunk] = hidden_pool.tile([P, PASSES, CHUNK], U8, align_bytes=64, tag="scales", name="scales")
-            quantise(grouped[:].rearrange("p r t -> p (r t)"), h_codes[chunk][:, g, :], h_scales[chunk][:, g, :])
+            quantise(
+                h_grouped[step][:].rearrange("p r t -> p (r t)")[:, PACK * first : PACK * (first + w)],
+                h_codes[chunk][:, g, first : first + w],
+                h_scales[chunk][:, g, first : first + w],
+            )
 
         def matmul2_pass(q, g):
             chunk, t = divmod(q, TILES_PER_CHUNK)
             if g == 0:
-                f_banks[q] = psum_f.tile([P, E], F32, tag="f", name="f_bank")
+                pool, tag = (psum_h, "h") if q >= LAST_CHUNK else (psum_f, "f")
+                f_banks[q] = pool.tile([P, E], F32, tag=tag, name="f_bank")
             tokens = slice(P * t, P * (t + 1))
             nc.tensor.matmul_mx(
                 out=f_banks[q][:],
@@ -237,13 +308,17 @@ def tile_swintransformerblock_pb_kernel(tc, y, w1, b1, w2, b2, ln2_g, ln2_b, out
             )
 
         def residual(q):
-            bank = psum_aux.tile([P, E], F32, tag="aux")
+            bank = psum_aux.tile([P, E], F32, tag="aux", name="r_bank")
             nc.tensor.matmul(out=bank[:], lhsT=ident_bf[:], rhs=y_sb[:, E * q : E * (q + 1)], start=True, stop=False)
             nc.tensor.matmul(out=bank[:], lhsT=ones_bf[:], rhs=b2_row[:], start=False, stop=True)
-            return bank
+            resid_banks[q] = bank
+
+        def copy_residual(q):
+            resid[q] = resid_pool.tile([P, E], F32, tag="resid", name="resid")
+            nc.scalar.copy(out=resid[q][:], in_=resid_banks[q][:])
 
         def add_residual(q):
-            summed[q] = norm_pool.tile([P, E], F32, tag="summed", name="summed")
+            summed[q] = summed_pool.tile([P, E], F32, tag="summed", name="summed")
             totals[q] = stat_pool.tile([P, 1], F32, tag="total", name="total")
             nc.vector.scalar_tensor_tensor(
                 out=summed[q][:], in0=f_banks[q][:], scalar=1.0, in1=resid[q][:],
@@ -255,106 +330,134 @@ def tile_swintransformerblock_pb_kernel(tc, y, w1, b1, w2, b2, ln2_g, ln2_b, out
             nc.vector.tensor_scalar_mul(out=neg_mean[q][:], in0=totals[q][:], scalar1=-1.0 / E)
 
         def centre(q):
-            centred[q] = norm_pool.tile([P, E], F32, tag="centred", name="centred")
+            centred[q] = centred_pool.tile([P, E], F32, tag="centred", name="centred")
             nc.vector.scalar_tensor_tensor(
                 out=centred[q][:], in0=summed[q][:], scalar=neg_mean[q][:], in1=gain_bf[:], op0=ALU.add, op1=ALU.mult
             )
 
         def sum_of_squares(q):
-            squares = norm_pool.tile([P, E], BF16, tag="squares")
+            squares = norm_pool.tile([P, E], BF16, tag="squares", name="squares")
             sums_of_squares[q] = stat_pool.tile([P, 1], F32, tag="sum_squares", name="sum_squares")
             nc.scalar.activation(
                 out=squares[:], in_=summed[q][:], func=ACT.Square, bias=neg_mean[q][:], accum_out=sums_of_squares[q][:]
             )
 
         def inverse_deviation(q):
-            padded = stat_pool.tile([P, 1], F32, tag="padded")
+            padded = stat_pool.tile([P, 1], F32, tag="padded", name="padded")
             nc.scalar.activation(
                 out=padded[:], in_=sums_of_squares[q][:], func=ACT.Identity, bias=eps_col[:], scale=1.0 / E
             )
-            inv_dev[q] = stat_pool.tile([P, 1], F32, tag="inv_dev", name="inv_dev")
-            nc.gpsimd.tensor_tensor(out=inv_dev[q][:], in0=padded[:], in1=neg_half[:], op=ALU.pow)
+            powers = stat_pool.tile([P, 1], F32, tag="powers", name="powers")
+            nc.gpsimd.tensor_tensor(out=powers[:], in0=padded[:], in1=neg_half[:], op=ALU.pow)
+            inv_dev[q] = powers[:]
 
         def scale_shift_store(q):
             ww, c = divmod(q, TILES_PER_CHUNK)
-            z = out_pool.tile([P, E], F32, tag="z")
+            z = out_pool.tile([P, E], F32, tag="z", name="z")
             nc.vector.scalar_tensor_tensor(
-                out=z[:], in0=centred[q][:], scalar=inv_dev[q][:], in1=shift_bf[:], op0=ALU.mult, op1=ALU.add
+                out=z[:], in0=centred[q][:], scalar=inv_dev[q], in1=shift_bf[:], op0=ALU.mult, op1=ALU.add
             )
             for x in range(2):
                 nc.sync.dma_start(out=out_view[ww, c, x], in_=z[x:P:2, :])
 
-        weight_groups = [(w1_words, PLANES * WORDS * g, WORDS, w1_codes, w1_scales, g) for g in range(PASSES)]
-        weight_groups += [(w2_words, PLANES * WORDS * g, WORDS, w2_codes, w2_scales, g) for g in range(PASSES)]
-        first_round = MATMUL2_LAG - len(weight_groups)
+        scalar_copy = nc.scalar.copy
+        vector_copy = nc.vector.tensor_copy
+        f_place, aux_place = (psum_f, "f"), (psum_aux, "aux")
 
-        weight_banks = []
-        y_banks = []
-        resid_banks = []
-        y_grouped = {}
-        for i in range(first_round, STEPS + SCALE_LAG):
-            q_resid, q_mm2, q_var, q_out = i - RESIDUAL_LAG, i - MATMUL2_LAG, i - VARIANCE_LAG, i - SCALE_LAG
-            if 0 <= i < STEPS:
-                gelu(i)
+        y_transposes(0, 0, aux_place)
+        y_transposes(0, 1, aux_place)
+        weight_transposes(0, [f_place, f_place])
+        y_copy(0, 0, scalar_copy)
+        y_copy(0, 1, vector_copy)
+        weight_copy(0, 0, scalar_copy)
+        weight_copy(0, 1, scalar_copy)
+        y_quantise(0)
+        weight_quantise(0)
+        spread_b1()
+        weight_transposes(1, [aux_place, aux_place])
+        for j in range(PLANES):
+            matmul1_bank(0, j)
+        weight_copy(1, 0, scalar_copy)
+        weight_copy(1, 1, vector_copy)
+        weight_quantise(1)
+        weight_transposes(2, [f_place, f_place])
+        weight_transposes(3, [aux_place, aux_place])
 
-            complete = []
-            for n, banks in weight_banks:
-                grouped = new_group()
-                nc.scalar.copy(out=pairs_of(grouped, 0), in_=banks[0][:].rearrange("p u c -> p c u"))
-                nc.vector.tensor_copy(out=pairs_of(grouped, 1), in_=banks[1][:].rearrange("p u c -> p c u"))
-                codes, scales, g = weight_groups[n][3:]
-                complete.append((grouped, codes, scales, g))
-            for chunk, half, bank in y_banks:
-                if half == 0:
-                    y_grouped[chunk] = new_group()
-                nc.scalar.copy(
-                    out=y_grouped[chunk][:]
-                    .bitcast(F32)
-                    .rearrange("p (c m u) -> p c m u", c=TILES_PER_CHUNK, u=2)[:, :, 64 * half : 64 * (half + 1), :],
-                    in_=bank[:].rearrange("p u (m c) -> p c m u", c=TILES_PER_CHUNK),
-                )
-                if half == 1:
-                    complete.append((y_grouped[chunk], y_codes, y_scales, chunk))
-            if 0 <= q_var < TILES:
+        transpose_weights = {0: [(4, f_place)], 1: [(5, f_place), (6, aux_place)], 2: [(7, f_place)]}
+        empty_weights = {0: [2, 3], 1: [4], 2: [5, 6], 3: [7]}
+        quantise_weights = {1: [2, 3], 2: [4], 3: [5, 6], 4: [7]}
+        transpose_y = {0: [(1, 0), (1, 1)]}
+        empty_y = {1: [(1, 0), (1, 1)]}
+        quantise_y = {2: 1}
+        for chunk in range(2, TOKENS // CHUNK):
+            for half in range(2):
+                transpose_y[PASSES * chunk - 5 + half] = [(chunk, half)]
+                empty_y[PASSES * chunk - 4 + half] = [(chunk, half)]
+            quantise_y[PASSES * chunk - 2] = chunk
+
+        def tile_at(i, lag):
+            return i - lag if 0 <= i - lag < TILES else None
+
+        for i in range(STEPS + SCALE_LAG):
+            live = i < STEPS
+            last = i == STEPS - 1
+            q_resid, q_copy, q_add = tile_at(i, RESIDUAL_LAG), tile_at(i, RESIDUAL_COPY_LAG), tile_at(i, ADD_LAG)
+            q_var, q_out = tile_at(i, VARIANCE_LAG), tile_at(i, SCALE_LAG)
+
+            if live:
+                for j in range(PLANES):
+                    gelu_bank(i, j)
+            for n in empty_weights.get(i, []):
+                weight_copy(n, 0, scalar_copy)
+            for chunk, half in empty_y.get(i, []):
+                y_copy(chunk, half, scalar_copy)
+            if q_var is not None:
                 sum_of_squares(q_var)
-            for q, bank in resid_banks:
-                resid[q] = resid_pool.tile([P, E], F32, tag="resid", name="resid")
-                nc.scalar.copy(out=resid[q][:], in_=bank[:])
-            if 0 <= q_var < TILES:
+            if q_copy is not None:
+                copy_residual(q_copy)
+            if q_var is not None:
                 inverse_deviation(q_var)
 
-            if 0 <= i < STEPS:
-                h_grouped = regroup(i)
-            for grouped, codes, scales, g in complete:
-                quantise(grouped[:], codes[:, columns(g)], scales[:, columns(g)])
+            for n in empty_weights.get(i, []):
+                weight_copy(n, 1, vector_copy)
+            for n in quantise_weights.get(i, []):
+                weight_quantise(n)
+            if i in quantise_y:
+                y_quantise(quantise_y[i])
+            if live:
+                regroup(i, 0)
 
             for k in range(PLANES):
-                if 0 <= i + 1 < STEPS:
-                    matmul1_pass(i + 1, k)
-                if 0 <= q_mm2 < TILES:
-                    matmul2_pass(q_mm2, k)
-            weight_banks = []
-            n = i - first_round
-            if n < len(weight_groups):
-                words, base, block_step = weight_groups[n][:3]
-                weight_banks = [(n, [transpose_half(words, base, block_step, half, psum_f, "f") for half in range(2)])]
-            y_banks = []
-            chunk, half = divmod(i + PASSES, PASSES)
-            if chunk < TOKENS // CHUNK and half < 2:
-                y_banks = [(chunk, half, transpose_half(y_words, TILES_PER_CHUNK * WORDS * chunk, WORDS, half, psum_aux, "aux"))]
-            resid_banks = []
-            if 0 <= q_resid < TILES:
-                resid_banks = [(q_resid, residual(q_resid))]
-            if i == first_round:
-                spread_b1()
+                if i + 1 < STEPS:
+                    matmul1_bank(i + 1, k)
+                if q_add is not None and q_add < LAST_CHUNK:
+                    matmul2_pass(q_add, k)
+            if last:
+                for q in range(LAST_CHUNK, TILES):
+                    for g in range(PASSES - 1):
+                        matmul2_pass(q, g)
+            for n, place in transpose_weights.get(i, []):
+                weight_transposes(n, [place, place])
+            for chunk, half in transpose_y.get(i, []):
+                y_transposes(chunk, half, aux_place)
+            if q_resid is not None:
+                residual(q_resid)
 
-            if 0 <= q_mm2 < TILES:
-                add_residual(q_mm2)
-            if 0 <= i < STEPS:
-                quantise_hidden(i, h_grouped)
-            if 0 <= q_mm2 < TILES:
-                negative_mean(q_mm2)
-            if 0 <= q_out < TILES:
+            if q_add is not None:
+                add_residual(q_add)
+            if live:
+                quantise_hidden(i, 0)
+            if last:
+                regroup(i, 1)
+                for q in range(LAST_CHUNK, LAST_CHUNK + 2):
+                    matmul2_pass(q, PASSES - 1)
+            if q_add is not None:
+                negative_mean(q_add)
+            if q_out is not None:
                 scale_shift_store(q_out)
-            if 0 <= q_mm2 < TILES:
-                centre(q_mm2)
+            if last:
+                quantise_hidden(i, 1)
+                for q in range(LAST_CHUNK + 2, TILES):
+                    matmul2_pass(q, PASSES - 1)
+            if q_add is not None:
+                centre(q_add)

@@ -100,7 +100,6 @@ def tile_swintransformerblock_pb_kernel(tc, y, w1, b1, w2, b2, ln2_g, ln2_b, out
         nc.vector.memset(ones_bf[:], 1.0)
         nc.vector.memset(eps_col[:], LN_EPS)
         nc.vector.memset(neg_half[:], -0.5)
-        nc.scalar.activation(out=warm_out[:], in_=warm[:], func=ACT.Gelu)
 
         w1_view = w1.rearrange("(gu p e2) k -> p gu (e2 k)", gu=F // (2 * P), p=P, e2=2)
         w1_slots = w1_sb[:].rearrange("p (gu n) -> p gu n", n=2 * E)
@@ -118,16 +117,14 @@ def tile_swintransformerblock_pb_kernel(tc, y, w1, b1, w2, b2, ln2_g, ln2_b, out
         def load_w2(g):
             nc.sync.dma_start(out=w2_slots[:, g], in_=w2_view[:, g])
 
-        def load_y(first_chunk, chunks):
+        def load_y(ww):
             for bw in range(WINDOW_ROWS):
-                nc.sync.dma_start(
-                    out=y_chunks[16 * bw : 16 * bw + 16, first_chunk : first_chunk + chunks, :],
-                    in_=y_view[bw, :, first_chunk : first_chunk + chunks, :],
-                )
+                nc.sync.dma_start(out=y_chunks[16 * bw : 16 * bw + 16, ww, :], in_=y_view[bw, :, ww, :])
 
         def load_y_win(ww):
             for w in range(2):
-                nc.sync.dma_start(out=y_win_chunks[64 * w : 64 * (w + 1), ww], in_=y_win_view[w, ww])
+                queue = nc.scalar if ww == 0 and w == 1 else nc.sync
+                queue.dma_start(out=y_win_chunks[64 * w : 64 * (w + 1), ww], in_=y_win_view[w, ww])
 
         nc.sync.dma_start(out=b1_rows[0:8, :], in_=b1.rearrange("(gu n) -> gu n", n=2 * P))
         make_identity(nc, ident[:])
@@ -137,16 +134,17 @@ def tile_swintransformerblock_pb_kernel(tc, y, w1, b1, w2, b2, ln2_g, ln2_b, out
         nc.gpsimd.dma_start(out=shift_bf[:], in_=ln2_b.partition_broadcast(P))
 
         load_y_win(0)
+        nc.scalar.activation(out=warm_out[:], in_=warm[:], func=ACT.Gelu)
         for g in range(PASSES):
             load_w1(g)
         load_y_win(1)
         for g in range(PASSES):
             load_w2(g)
-        load_y(0, 2)
+        load_y(0)
         load_y_win(2)
-        load_y(2, WINDOW_COLS - 2)
+        load_y(1)
         load_y_win(3)
-        load_y_win(4)
+        late_loads = {2: [(load_y, 2)], 5: [(load_y_win, 4)], 7: [(load_y, 3)], 11: [(load_y, 4)]}
 
         def transpose_half(words, base, half, pool, tag):
             bank = pool.tile([P, 2, 2 * P], F32, tag=tag, name="words_bank")
@@ -403,6 +401,9 @@ def tile_swintransformerblock_pb_kernel(tc, y, w1, b1, w2, b2, ln2_g, ln2_b, out
             last = i == STEPS - 1
             q_resid, q_copy, q_add = tile_at(i, RESIDUAL_LAG), tile_at(i, RESIDUAL_COPY_LAG), tile_at(i, ADD_LAG)
             q_var, q_out = tile_at(i, VARIANCE_LAG), tile_at(i, SCALE_LAG)
+
+            for load, ww in late_loads.get(i, []):
+                load(ww)
 
             if live:
                 for j in range(PLANES):

@@ -85,6 +85,8 @@ def tile_swintransformerblock_pb_kernel(tc, y, w1, b1, w2, b2, ln2_g, ln2_b, out
         ones_bf = keep.tile([P, P], BF16)
         b2_row = keep.tile([P, E], BF16)
         eps_col = keep.tile([P, 1], F32)
+        gain_row = keep.tile([P, E], BF16)
+        shift_row = keep.tile([P, E], BF16)
         gain_bf = keep.tile([P, E], BF16)
         shift_bf = keep.tile([P, E], BF16)
         warm = keep.tile([P, 1], F32)
@@ -96,6 +98,8 @@ def tile_swintransformerblock_pb_kernel(tc, y, w1, b1, w2, b2, ln2_g, ln2_b, out
 
         nc.vector.memset(warm[:], 0.0)
         nc.vector.memset(b1_rows[:], 0.0)
+        nc.vector.memset(gain_row[:], 0.0)
+        nc.vector.memset(shift_row[:], 0.0)
         nc.vector.memset(b2_row[:], 0.0)
         nc.vector.memset(ones_bf[:], 1.0)
         nc.vector.memset(eps_col[:], LN_EPS)
@@ -126,16 +130,17 @@ def tile_swintransformerblock_pb_kernel(tc, y, w1, b1, w2, b2, ln2_g, ln2_b, out
                 queue = nc.scalar if ww == 0 and w == 1 else nc.sync
                 queue.dma_start(out=y_win_chunks[64 * w : 64 * (w + 1), ww], in_=y_win_view[w, ww])
 
-        nc.sync.dma_start(out=b1_rows[0:8, :], in_=b1.rearrange("(gu n) -> gu n", n=2 * P))
         make_identity(nc, ident[:])
         make_identity(nc, ident_bf[:])
         nc.gpsimd.dma_start(out=b2_row[0:1, :], in_=b2.rearrange("(o e) -> o e", o=1))
-        nc.gpsimd.dma_start(out=gain_bf[:], in_=ln2_g.partition_broadcast(P))
-        nc.gpsimd.dma_start(out=shift_bf[:], in_=ln2_b.partition_broadcast(P))
 
         load_y_win(0)
+        load_w1(0)
+        nc.sync.dma_start(out=b1_rows[0:8, :], in_=b1.rearrange("(gu n) -> gu n", n=2 * P))
+        nc.sync.dma_start(out=gain_row[0:1, :], in_=ln2_g.rearrange("(o e) -> o e", o=1))
+        nc.sync.dma_start(out=shift_row[0:1, :], in_=ln2_b.rearrange("(o e) -> o e", o=1))
         nc.scalar.activation(out=warm_out[:], in_=warm[:], func=ACT.Gelu)
-        for g in range(PASSES):
+        for g in range(1, PASSES):
             load_w1(g)
         load_y_win(1)
         for g in range(PASSES):
@@ -213,6 +218,11 @@ def tile_swintransformerblock_pb_kernel(tc, y, w1, b1, w2, b2, ln2_g, ln2_b, out
             nc.tensor.transpose(out=bank[:, 0:P], in_=b1_rows[:].bitcast(F32), identity=ident[:])
             nc.vector.tensor_copy(out=b1_pairs[:].bitcast(F32), in_=bank[:, 0 : F // (2 * P)])
             nc.vector.tensor_copy(out=b1_col[:], in_=b1_pairs[:])
+
+        def spread_row(row, spread):
+            bank = psum_h.tile([P, CHUNK], F32, tag="h", name="row_bank")
+            nc.tensor.matmul(out=bank[:], lhsT=ones_bf[:], rhs=row[:], start=True, stop=True)
+            nc.scalar.copy(out=spread[:], in_=bank[:])
 
         h_banks = {}
         h_planes = {}
@@ -372,6 +382,8 @@ def tile_swintransformerblock_pb_kernel(tc, y, w1, b1, w2, b2, ln2_g, ln2_b, out
         y_quantise(0)
         weight_quantise(0)
         spread_b1()
+        spread_row(gain_row, gain_bf)
+        spread_row(shift_row, shift_bf)
         weight_transposes(1, [aux_place, aux_place])
         for j in range(PLANES):
             matmul1_bank(0, j)

@@ -127,15 +127,19 @@ def tile_swintransformerblock_pb_kernel(tc, y, w1, b1, w2, b2, ln2_g, ln2_b, out
 
         def load_y_win(ww):
             for w in range(2):
-                queue = nc.scalar if ww == 0 and w == 1 else nc.sync
-                queue.dma_start(out=y_win_chunks[64 * w : 64 * (w + 1), ww], in_=y_win_view[w, ww])
+                nc.sync.dma_start(out=y_win_chunks[64 * w : 64 * (w + 1), ww], in_=y_win_view[w, ww])
 
         make_identity(nc, ident[:])
         make_identity(nc, ident_bf[:])
-        nc.gpsimd.dma_start(out=b2_row[0:1, :], in_=b2.rearrange("(o e) -> o e", o=1))
 
-        load_y_win(0)
-        load_w1(0)
+        for half in range(2):
+            blocks = slice(2 * half, 2 * half + 2)
+            for w, queue in enumerate([nc.sync, nc.scalar]):
+                queue.dma_start(
+                    out=y_win_chunks[64 * w : 64 * (w + 1), 0, blocks], in_=y_win_view[w, 0][:, blocks]
+                )
+        for gu in range(2):
+            nc.sync.dma_start(out=w1_slots[:, gu : gu + 1, :], in_=w1_view[:, gu : gu + 1, :])
         nc.sync.dma_start(out=b1_rows[0:8, :], in_=b1.rearrange("(gu n) -> gu n", n=2 * P))
         nc.sync.dma_start(out=gain_row[0:1, :], in_=ln2_g.rearrange("(o e) -> o e", o=1))
         nc.sync.dma_start(out=shift_row[0:1, :], in_=ln2_b.rearrange("(o e) -> o e", o=1))
@@ -145,6 +149,7 @@ def tile_swintransformerblock_pb_kernel(tc, y, w1, b1, w2, b2, ln2_g, ln2_b, out
         load_y_win(1)
         for g in range(PASSES):
             load_w2(g)
+        nc.sync.dma_start(out=b2_row[0:1, :], in_=b2.rearrange("(o e) -> o e", o=1))
         load_y(0)
         load_y_win(2)
         load_y(1)
@@ -176,11 +181,9 @@ def tile_swintransformerblock_pb_kernel(tc, y, w1, b1, w2, b2, ln2_g, ln2_b, out
         weight_banks = {}
         weight_grouped = {}
 
-        def weight_transposes(n, places):
+        def weight_transposes(n, half, place):
             words, codes, scales, g = weights[n]
-            weight_banks[n] = [
-                transpose_half(words, PLANES * WORDS * g, half, *places[half]) for half in range(2)
-            ]
+            weight_banks[(n, half)] = transpose_half(words, PLANES * WORDS * g, half, *place)
 
         def weight_copy(n, half, engine_copy):
             if n not in weight_grouped:
@@ -188,11 +191,16 @@ def tile_swintransformerblock_pb_kernel(tc, y, w1, b1, w2, b2, ln2_g, ln2_b, out
             pairs = weight_grouped[n][:].bitcast(F32)[:, CHUNK * half : CHUNK * (half + 1)].rearrange(
                 "p (c u) -> p c u", u=2
             )
-            engine_copy(out=pairs, in_=weight_banks[n][half][:].rearrange("p u c -> p c u"))
+            engine_copy(out=pairs, in_=weight_banks[(n, half)][:].rearrange("p u c -> p c u"))
 
         def weight_quantise(n):
             words, codes, scales, g = weights[n]
             quantise(weight_grouped[n][:], codes[:, columns(g)], scales[:, columns(g)])
+
+        def weight_quantise_half(n, half):
+            words, codes, scales, g = weights[n]
+            rows = slice(CHUNK * g + HALF * half, CHUNK * g + HALF * (half + 1))
+            quantise(weight_grouped[n][:, PACK * HALF * half : PACK * HALF * (half + 1)], codes[:, rows], scales[:, rows])
 
         y_banks = {}
         y_grouped = {}
@@ -219,10 +227,10 @@ def tile_swintransformerblock_pb_kernel(tc, y, w1, b1, w2, b2, ln2_g, ln2_b, out
             nc.vector.tensor_copy(out=b1_pairs[:].bitcast(F32), in_=bank[:, 0 : F // (2 * P)])
             nc.vector.tensor_copy(out=b1_col[:], in_=b1_pairs[:])
 
-        def spread_row(row, spread):
-            bank = psum_h.tile([P, CHUNK], F32, tag="h", name="row_bank")
+        def spread_row(row):
+            bank = psum_aux.tile([P, CHUNK], F32, tag="aux", name="row_bank")
             nc.tensor.matmul(out=bank[:], lhsT=ones_bf[:], rhs=row[:], start=True, stop=True)
-            nc.scalar.copy(out=spread[:], in_=bank[:])
+            return bank
 
         h_banks = {}
         h_planes = {}
@@ -280,9 +288,9 @@ def tile_swintransformerblock_pb_kernel(tc, y, w1, b1, w2, b2, ln2_g, ln2_b, out
                     bias=b1_col[:, plane : plane + 1],
                 )
 
-        def regroup(step, piece):
+        def regroup(step, piece, engine_copy):
             first, w = pieces(step)[piece]
-            nc.vector.tensor_copy(
+            engine_copy(
                 out=h_grouped[step][:, first : first + w, :].rearrange("p (c i) t -> p c t i", i=4),
                 in_=h_planes[step][:, :, first : first + w].rearrange("p t (c i) -> p c t i", i=4),
             )
@@ -374,24 +382,37 @@ def tile_swintransformerblock_pb_kernel(tc, y, w1, b1, w2, b2, ln2_g, ln2_b, out
 
         y_transposes(0, 0, aux_place)
         y_transposes(0, 1, aux_place)
-        weight_transposes(0, [f_place, f_place])
+        weight_transposes(0, 0, f_place)
+        weight_transposes(0, 1, f_place)
         y_copy(0, 0, scalar_copy)
         y_copy(0, 1, vector_copy)
         weight_copy(0, 0, scalar_copy)
-        weight_copy(0, 1, scalar_copy)
         y_quantise(0)
-        weight_quantise(0)
+        weight_quantise_half(0, 0)
+        weight_copy(0, 1, scalar_copy)
+        weight_quantise_half(0, 1)
         spread_b1()
-        spread_row(gain_row, gain_bf)
-        spread_row(shift_row, shift_bf)
-        weight_transposes(1, [aux_place, aux_place])
-        for j in range(PLANES):
-            matmul1_bank(0, j)
+        gain_bank = spread_row(gain_row)
+        shift_bank = spread_row(shift_row)
+        scalar_copy(out=gain_bf[:], in_=gain_bank[:])
+        vector_copy(out=shift_bf[:], in_=shift_bank[:])
+        matmul1_bank(0, 0)
+        matmul1_bank(0, 1)
+        weight_transposes(1, 0, aux_place)
+        weight_transposes(1, 1, aux_place)
+        matmul1_bank(0, 2)
+        matmul1_bank(0, 3)
+        gelu_bank(0, 0)
+        gelu_bank(0, 1)
         weight_copy(1, 0, scalar_copy)
         weight_copy(1, 1, vector_copy)
         weight_quantise(1)
-        weight_transposes(2, [f_place, f_place])
-        weight_transposes(3, [aux_place, aux_place])
+        for half in range(2):
+            weight_transposes(2, half, f_place)
+        for half in range(2):
+            weight_transposes(3, half, aux_place)
+        gelu_bank(0, 2)
+        gelu_bank(0, 3)
 
         transpose_weights = {0: [(4, f_place)], 1: [(5, f_place), (6, aux_place)], 2: [(7, f_place)]}
         empty_weights = {0: [2, 3], 1: [4], 2: [5, 6], 3: [7]}
@@ -417,9 +438,11 @@ def tile_swintransformerblock_pb_kernel(tc, y, w1, b1, w2, b2, ln2_g, ln2_b, out
             for load, ww in late_loads.get(i, []):
                 load(ww)
 
-            if live:
+            if 0 < i < STEPS:
                 for j in range(PLANES):
                     gelu_bank(i, j)
+            if last:
+                regroup(i, 1, scalar_copy)
             for n in empty_weights.get(i, []):
                 weight_copy(n, 0, scalar_copy)
             for chunk, half in empty_y.get(i, []):
@@ -438,7 +461,7 @@ def tile_swintransformerblock_pb_kernel(tc, y, w1, b1, w2, b2, ln2_g, ln2_b, out
             if i in quantise_y:
                 y_quantise(quantise_y[i])
             if live:
-                regroup(i, 0)
+                regroup(i, 0, vector_copy)
 
             for k in range(PLANES):
                 if i + 1 < STEPS:
@@ -450,7 +473,8 @@ def tile_swintransformerblock_pb_kernel(tc, y, w1, b1, w2, b2, ln2_g, ln2_b, out
                     for g in range(PASSES - 1):
                         matmul2_pass(q, g)
             for n, place in transpose_weights.get(i, []):
-                weight_transposes(n, [place, place])
+                for half in range(2):
+                    weight_transposes(n, half, place)
             for chunk, half in transpose_y.get(i, []):
                 y_transposes(chunk, half, aux_place)
             if q_resid is not None:
@@ -461,7 +485,6 @@ def tile_swintransformerblock_pb_kernel(tc, y, w1, b1, w2, b2, ln2_g, ln2_b, out
             if live:
                 quantise_hidden(i, 0)
             if last:
-                regroup(i, 1)
                 for q in range(LAST_CHUNK, LAST_CHUNK + 2):
                     matmul2_pass(q, PASSES - 1)
             if q_add is not None:

@@ -33,6 +33,7 @@ WORD_HALF = 2 * P
 
 LAST_CHUNK = TILES - TILES_PER_CHUNK
 HALF = CHUNK // 2
+PE_ADDED = (18, 19)
 
 RESIDUAL_LAG = 2
 RESIDUAL_COPY_LAG = 3
@@ -134,10 +135,8 @@ def tile_swintransformerblock_pb_kernel(tc, y, w1, b1, w2, b2, ln2_g, ln2_b, out
 
         for half in range(2):
             blocks = slice(2 * half, 2 * half + 2)
-            for w, queue in enumerate([nc.sync, nc.scalar]):
-                queue.dma_start(
-                    out=y_win_chunks[64 * w : 64 * (w + 1), 0, blocks], in_=y_win_view[w, 0][:, blocks]
-                )
+            nc.sync.dma_start(out=y_win_chunks[0:64, 0, blocks], in_=y_win_view[0, 0][:, blocks])
+            nc.scalar.dma_start(out=y_win_chunks[64:P, 0, blocks], in_=y_win_view[1, 0][:, blocks])
         for gu in range(2):
             nc.sync.dma_start(out=w1_slots[:, gu : gu + 1, :], in_=w1_view[:, gu : gu + 1, :])
         nc.sync.dma_start(out=b1_rows[0:8, :], in_=b1.rearrange("(gu n) -> gu n", n=2 * P))
@@ -154,7 +153,6 @@ def tile_swintransformerblock_pb_kernel(tc, y, w1, b1, w2, b2, ln2_g, ln2_b, out
         load_y_win(2)
         load_y(1)
         load_y_win(3)
-        late_loads = {2: [(load_y, 2)], 5: [(load_y_win, 4)], 7: [(load_y, 3)], 11: [(load_y, 4)]}
 
         def transpose_half(words, base, half, pool, tag):
             bank = pool.tile([P, 2, 2 * P], F32, tag=tag, name="words_bank")
@@ -239,6 +237,7 @@ def tile_swintransformerblock_pb_kernel(tc, y, w1, b1, w2, b2, ln2_g, ln2_b, out
         h_scales = {}
         f_banks = {}
         resid_banks = {}
+        f_copies = {}
         resid = {}
         summed = {}
         totals = {}
@@ -328,6 +327,22 @@ def tile_swintransformerblock_pb_kernel(tc, y, w1, b1, w2, b2, ln2_g, ln2_b, out
             nc.tensor.matmul(out=bank[:], lhsT=ident_bf[:], rhs=y_sb[:, E * q : E * (q + 1)], start=True, stop=False)
             nc.tensor.matmul(out=bank[:], lhsT=ones_bf[:], rhs=b2_row[:], start=False, stop=True)
             resid_banks[q] = bank
+
+        def copy_f(q):
+            f_copies[q] = summed_pool.tile([P, E], F32, tag="f_copy", name="f_copy")
+            nc.scalar.copy(out=f_copies[q][:], in_=f_banks[q][:])
+
+        def add_on_tensor(q):
+            bank = psum_f.tile([P, E], F32, tag="f", name="r_bank")
+            nc.tensor.matmul(out=bank[:], lhsT=ident_bf[:], rhs=y_sb[:, E * q : E * (q + 1)], start=True, stop=False)
+            nc.tensor.matmul(out=bank[:], lhsT=ones_bf[:], rhs=b2_row[:], start=False, stop=False)
+            nc.tensor.matmul(out=bank[:], lhsT=ident[:], rhs=f_copies[q][:], start=False, stop=True)
+            summed[q] = bank
+
+        def total(q):
+            spare = norm_pool.tile([P, E], BF16, tag="squares", name="spare")
+            totals[q] = stat_pool.tile([P, 1], F32, tag="total", name="total")
+            nc.scalar.activation(out=spare[:], in_=summed[q][:], func=ACT.Identity, accum_out=totals[q][:])
 
         def copy_residual(q):
             resid[q] = resid_pool.tile([P, E], F32, tag="resid", name="resid")
@@ -435,8 +450,10 @@ def tile_swintransformerblock_pb_kernel(tc, y, w1, b1, w2, b2, ln2_g, ln2_b, out
             q_resid, q_copy, q_add = tile_at(i, RESIDUAL_LAG), tile_at(i, RESIDUAL_COPY_LAG), tile_at(i, ADD_LAG)
             q_var, q_out = tile_at(i, VARIANCE_LAG), tile_at(i, SCALE_LAG)
 
-            for load, ww in late_loads.get(i, []):
-                load(ww)
+            if i == 5:
+                load_y_win(4)
+            if i in (2, 7, 11):
+                load_y({2: 2, 7: 3, 11: 4}[i])
 
             if 0 < i < STEPS:
                 for j in range(PLANES):
@@ -449,10 +466,17 @@ def tile_swintransformerblock_pb_kernel(tc, y, w1, b1, w2, b2, ln2_g, ln2_b, out
                 y_copy(chunk, half, scalar_copy)
             if q_var is not None:
                 sum_of_squares(q_var)
-            if q_copy is not None:
+            if q_copy is not None and q_copy not in PE_ADDED:
                 copy_residual(q_copy)
             if q_var is not None:
                 inverse_deviation(q_var)
+            if i == STEPS:
+                for q in PE_ADDED:
+                    copy_f(q)
+                for q in PE_ADDED:
+                    add_on_tensor(q)
+            if q_copy in PE_ADDED:
+                total(q_copy)
 
             for n in empty_weights.get(i, []):
                 weight_copy(n, 1, vector_copy)
@@ -477,10 +501,10 @@ def tile_swintransformerblock_pb_kernel(tc, y, w1, b1, w2, b2, ln2_g, ln2_b, out
                     weight_transposes(n, half, place)
             for chunk, half in transpose_y.get(i, []):
                 y_transposes(chunk, half, aux_place)
-            if q_resid is not None:
+            if q_resid is not None and q_resid not in PE_ADDED:
                 residual(q_resid)
 
-            if q_add is not None:
+            if q_add is not None and q_add not in PE_ADDED:
                 add_residual(q_add)
             if live:
                 quantise_hidden(i, 0)

from contextlib import ExitStack

import concourse.mybir as mybir
from concourse.masks import make_identity

F32 = mybir.dt.float32
BF16 = mybir.dt.bfloat16
U32 = mybir.dt.uint32
U8 = mybir.dt.uint8
FP8X4 = mybir.dt.float8_e4m3fn_x4
ACT = mybir.ActivationFunctionType
ALU = mybir.AluOpType

P = 128
PACK = 4
E = 512
F = 2048
PASSES = F // (P * PACK)
PLANES = PACK
TOKENS = 2560
TILES = TOKENS // P
CHUNK = 512
TILES_PER_CHUNK = CHUNK // P
STEPS = (TOKENS // CHUNK) * PASSES
WINDOW_ROWS = 8
WINDOW_COLS = 5
LN_EPS = 1e-5
WORDS = E // 2

FLOPS = 2 * TOKENS * E * F * 2

WORD_HALF = 2 * P

LAST_CHUNK = TILES - TILES_PER_CHUNK
HALF = CHUNK // 2
PE_ADDED = (18, 19)

RESIDUAL_LAG = 2
RESIDUAL_COPY_LAG = 3
ADD_LAG = 4
VARIANCE_LAG = 5
SCALE_LAG = 6


def tile_swintransformerblock_pb_kernel(tc, y, w1, b1, w2, b2, ln2_g, ln2_b, out):
    nc = tc.nc

    y_view = y.flatten_outer_dims().rearrange(
        "(bw ww rx c) e -> bw rx ww (c e)", bw=WINDOW_ROWS, ww=WINDOW_COLS, rx=16, c=TILES_PER_CHUNK
    )
    out_view = out.flatten_outer_dims().rearrange(
        "(bwr ww x c) e -> ww c x bwr e", bwr=64, ww=WINDOW_COLS, x=2, c=TILES_PER_CHUNK
    )

    with ExitStack() as ctx:
        keep = ctx.enter_context(tc.tile_pool(name="keep", bufs=1))
        group_pool = ctx.enter_context(tc.tile_pool(name="group", bufs=4))
        plane_pool = ctx.enter_context(tc.tile_pool(name="plane", bufs=3))
        hidden_pool = ctx.enter_context(tc.tile_pool(name="hidden", bufs=2))
        resid_pool = ctx.enter_context(tc.tile_pool(name="resid", bufs=3))
        summed_pool = ctx.enter_context(tc.tile_pool(name="summed", bufs=3))
        norm_pool = ctx.enter_context(tc.tile_pool(name="norm", bufs=2))
        centred_pool = ctx.enter_context(tc.tile_pool(name="centred", bufs=5))
        out_pool = ctx.enter_context(tc.tile_pool(name="out", bufs=4))
        stat_pool = ctx.enter_context(tc.tile_pool(name="stat", bufs=4))
        psum_h = ctx.enter_context(tc.psum_pool(name="psum_h", bufs=4))
        psum_f = ctx.enter_context(tc.psum_pool(name="psum_f", bufs=2))
        psum_aux = ctx.enter_context(tc.psum_pool(name="psum_aux", bufs=2))
        ctx.enter_context(tc.manual_schedule())

        y_sb = keep.tile([P, TILES * E], BF16)
        y_win = keep.tile([P, TILES * E], BF16)
        w1_sb = keep.tile([P, (F // P) * E], BF16)
        w2_sb = keep.tile([P, (E // P) * F], BF16)
        y_codes = keep.tile([P, TOKENS], U32, align_bytes=64)
        y_scales = keep.tile([P, TOKENS], U8, align_bytes=64)
        w1_codes = keep.tile([P, F], U32, align_bytes=64)
        w1_scales = keep.tile([P, F], U8, align_bytes=64)
        w2_codes = keep.tile([P, PASSES * E], U32, align_bytes=64)
        w2_scales = keep.tile([P, PASSES * E], U8, align_bytes=64)
        ident = keep.tile([P, P], F32)
        ident_bf = keep.tile([P, P], BF16)
        b1_rows = keep.tile([P, 2 * P], BF16)
        b1_pairs = keep.tile([P, F // P], BF16)
        b1_col = keep.tile([P, F // P], F32)
        ones_bf = keep.tile([P, P], BF16)
        b2_row = keep.tile([P, E], BF16)
        eps_col = keep.tile([P, 1], F32)
        gain_row = keep.tile([P, E], BF16)
        shift_row = keep.tile([P, E], BF16)
        gain_bf = keep.tile([P, E], BF16)
        shift_bf = keep.tile([P, E], BF16)
        warm = keep.tile([P, 1], F32)
        warm_out = keep.tile([P, 1], F32)
        neg_half = keep.tile([P, 1], F32)

        def columns(i):
            return slice(CHUNK * i, CHUNK * (i + 1))

        nc.vector.memset(warm[:], 0.0)
        nc.vector.memset(b1_rows[:], 0.0)
        nc.vector.memset(gain_row[:], 0.0)
        nc.vector.memset(shift_row[:], 0.0)
        nc.vector.memset(b2_row[:], 0.0)
        nc.vector.memset(ones_bf[:], 1.0)
        nc.vector.memset(eps_col[:], LN_EPS)
        nc.vector.memset(neg_half[:], -0.5)

        w1_view = w1.rearrange("(gu p e2) k -> p gu (e2 k)", gu=F // (2 * P), p=P, e2=2)
        w1_slots = w1_sb[:].rearrange("p (gu n) -> p gu n", n=2 * E)
        w2_view = w2.rearrange("(ec p) (g f) -> p g ec f", p=P, g=PASSES)
        w2_slots = w2_sb[:].rearrange("p (g ec f) -> p g ec f", g=PASSES, f=P * PACK)
        y_chunks = y_sb[:].rearrange("p (ww n) -> p ww n", ww=WINDOW_COLS)
        y_win_view = y.flatten_outer_dims().rearrange(
            "(bwp w ww n) e -> w ww n bwp e", bwp=WINDOW_ROWS // 2, w=2, ww=WINDOW_COLS
        )
        y_win_chunks = y_win[:].rearrange("p (ww bwp e) -> p ww bwp e", ww=WINDOW_COLS, e=E)

        def load_w1(g):
            nc.sync.dma_start(out=w1_slots[:, 2 * g : 2 * g + 2, :], in_=w1_view[:, 2 * g : 2 * g + 2, :])

        def load_w2(g):
            nc.sync.dma_start(out=w2_slots[:, g], in_=w2_view[:, g])

        def load_y(ww):
            for bw in range(WINDOW_ROWS):
                nc.sync.dma_start(out=y_chunks[16 * bw : 16 * bw + 16, ww, :], in_=y_view[bw, :, ww, :])

        def load_y_win(ww):
            for w in range(2):
                nc.sync.dma_start(out=y_win_chunks[64 * w : 64 * (w + 1), ww], in_=y_win_view[w, ww])

        make_identity(nc, ident[:])
        make_identity(nc, ident_bf[:])

        for half in range(2):
            blocks = slice(2 * half, 2 * half + 2)
            nc.sync.dma_start(out=y_win_chunks[0:64, 0, blocks], in_=y_win_view[0, 0][:, blocks])
            nc.scalar.dma_start(out=y_win_chunks[64:P, 0, blocks], in_=y_win_view[1, 0][:, blocks])
        for gu in range(2):
            nc.sync.dma_start(out=w1_slots[:, gu : gu + 1, :], in_=w1_view[:, gu : gu + 1, :])
        nc.sync.dma_start(out=b1_rows[0:8, :], in_=b1.rearrange("(gu n) -> gu n", n=2 * P))
        nc.sync.dma_start(out=gain_row[0:1, :], in_=ln2_g.rearrange("(o e) -> o e", o=1))
        nc.sync.dma_start(out=shift_row[0:1, :], in_=ln2_b.rearrange("(o e) -> o e", o=1))
        nc.scalar.activation(out=warm_out[:], in_=warm[:], func=ACT.Gelu)
        for g in range(1, PASSES):
            load_w1(g)
        load_y_win(1)
        for g in range(PASSES):
            load_w2(g)
        nc.sync.dma_start(out=b2_row[0:1, :], in_=b2.rearrange("(o e) -> o e", o=1))
        load_y(0)
        load_y_win(2)
        load_y(1)
        load_y_win(3)

        def transpose_half(words, base, half, pool, tag):
            bank = pool.tile([P, 2, 2 * P], F32, tag=tag, name="words_bank")
            for b in range(2):
                for u in range(2):
                    first = base + WORDS * (2 * half + b) + P * u
                    nc.tensor.transpose(
                        out=bank[:, u, P * b : P * (b + 1)], in_=words[:, first : first + P], identity=ident[:]
                    )
            return bank

        def new_group():
            return group_pool.tile([P, CHUNK * PACK], BF16, align_bytes=64, tag="grouped", name="grouped")

        def quantise(grouped, codes, scales):
            nc.vector.quantize_mx(out=codes.bitcast(FP8X4), scales=scales, in_=grouped)

        y_words = y_win[:].bitcast(F32)
        w1_words = w1_sb[:].bitcast(F32)
        w2_words = w2_sb[:].bitcast(F32)

        weights = [(w1_words, w1_codes, w1_scales, g) for g in range(PASSES)]
        weights += [(w2_words, w2_codes, w2_scales, g) for g in range(PASSES)]
        weight_banks = {}
        weight_grouped = {}

        def weight_transposes(n, half, place):
            words, codes, scales, g = weights[n]
            weight_banks[(n, half)] = transpose_half(words, PLANES * WORDS * g, half, *place)

        def weight_copy(n, half, engine_copy):
            if n not in weight_grouped:
                weight_grouped[n] = new_group()
            pairs = weight_grouped[n][:].bitcast(F32)[:, CHUNK * half : CHUNK * (half + 1)].rearrange(
                "p (c u) -> p c u", u=2
            )
            engine_copy(out=pairs, in_=weight_banks[(n, half)][:].rearrange("p u c -> p c u"))

        def weight_quantise(n):
            words, codes, scales, g = weights[n]
            quantise(weight_grouped[n][:], codes[:, columns(g)], scales[:, columns(g)])

        def weight_quantise_half(n, half):
            words, codes, scales, g = weights[n]
            rows = slice(CHUNK * g + HALF * half, CHUNK * g + HALF * (half + 1))
            quantise(weight_grouped[n][:, PACK * HALF * half : PACK * HALF * (half + 1)], codes[:, rows], scales[:, rows])

        y_banks = {}
        y_grouped = {}

        def y_transposes(chunk, half, place):
            y_banks[(chunk, half)] = transpose_half(y_words, TILES_PER_CHUNK * WORDS * chunk, half, *place)

        def y_copy(chunk, half, engine_copy):
            if chunk not in y_grouped:
                y_grouped[chunk] = new_group()
            engine_copy(
                out=y_grouped[chunk][:]
                .bitcast(F32)
                .rearrange("p (c m u) -> p c m u", c=TILES_PER_CHUNK, u=2)[:, :, 64 * half : 64 * (half + 1), :],
                in_=y_banks[(chunk, half)][:].rearrange("p u (m c) -> p c m u", c=TILES_PER_CHUNK),
            )

        def y_quantise(chunk):
            quantise(y_grouped[chunk][:], y_codes[:, columns(chunk)], y_scales[:, columns(chunk)])

        def spread_b1():
            bank = psum_h.tile([P, CHUNK], F32, tag="h", name="b1_bank")
            nc.tensor.transpose(out=bank[:, 0:P], in_=b1_rows[:].bitcast(F32), identity=ident[:])
            nc.vector.tensor_copy(out=b1_pairs[:].bitcast(F32), in_=bank[:, 0 : F // (2 * P)])
            nc.vector.tensor_copy(out=b1_col[:], in_=b1_pairs[:])

        def spread_row(row):
            bank = psum_aux.tile([P, CHUNK], F32, tag="aux", name="row_bank")
            nc.tensor.matmul(out=bank[:], lhsT=ones_bf[:], rhs=row[:], start=True, stop=True)
            return bank

        h_banks = {}
        h_planes = {}
        h_grouped = {}
        h_codes = {}
        h_scales = {}
        f_banks = {}
        resid_banks = {}
        f_copies = {}
        resid = {}
        summed = {}
        totals = {}
        neg_mean = {}
        centred = {}
        sums_of_squares = {}
        inv_dev = {}

        def pieces(step):
            return [(0, HALF), (HALF, HALF)] if step == STEPS - 1 else [(0, CHUNK)]

        def step_passes(step, j):
            passes = [(first, w, k) for first, w in pieces(step) for k in range(PLANES)]
            per_bank = len(passes) // PLANES
            return passes[per_bank * j : per_bank * (j + 1)]

        def matmul1_bank(step, j):
            chunk, g = divmod(step, PASSES)
            bank = psum_h.tile([P, CHUNK], F32, tag="h", name="h_bank")
            for n, (first, w, k) in enumerate(step_passes(step, j)):
                plane = slice(P * (PLANES * g + k), P * (PLANES * g + k + 1))
                tokens = slice(CHUNK * chunk + first, CHUNK * chunk + first + w)
                nc.tensor.matmul_mx(
                    out=bank[:, w * n : w * (n + 1)],
                    lhsT=w1_codes[:, plane].bitcast(FP8X4),
                    lhsT_scale=w1_scales[:, plane],
                    rhs=y_codes[:, tokens].bitcast(FP8X4),
                    rhs_scale=y_scales[:, tokens],
                    start=True,
                    stop=True,
                )
            h_banks[(step, j)] = bank

        def gelu_bank(step, j):
            chunk, g = divmod(step, PASSES)
            if j == 0:
                h_planes[step] = plane_pool.tile([P, PLANES, CHUNK], BF16, tag="planes", name="planes")
                h_grouped[step] = group_pool.tile(
                    [P, CHUNK, PACK], BF16, align_bytes=64, tag="h_grouped", name="h_grouped"
                )
            for n, (first, w, k) in enumerate(step_passes(step, j)):
                plane = PLANES * g + k
                nc.scalar.activation(
                    out=h_planes[step][:, k, first : first + w],
                    in_=h_banks[(step, j)][:, w * n : w * (n + 1)],
                    func=ACT.Gelu,
                    bias=b1_col[:, plane : plane + 1],
                )

        def regroup(step, piece, engine_copy):
            first, w = pieces(step)[piece]
            engine_copy(
                out=h_grouped[step][:, first : first + w, :].rearrange("p (c i) t -> p c t i", i=4),
                in_=h_planes[step][:, :, first : first + w].rearrange("p t (c i) -> p c t i", i=4),
            )

        def quantise_hidden(step, piece):
            chunk, g = divmod(step, PASSES)
            first, w = pieces(step)[piece]
            if g == 0 and piece == 0:
                h_codes[chunk] = hidden_pool.tile([P, PASSES, CHUNK], U32, align_bytes=64, tag="codes", name="codes")
                h_scales[chunk] = hidden_pool.tile([P, PASSES, CHUNK], U8, align_bytes=64, tag="scales", name="scales")
            quantise(
                h_grouped[step][:].rearrange("p r t -> p (r t)")[:, PACK * first : PACK * (first + w)],
                h_codes[chunk][:, g, first : first + w],
                h_scales[chunk][:, g, first : first + w],
            )

        def matmul2_pass(q, g):
            chunk, t = divmod(q, TILES_PER_CHUNK)
            if g == 0:
                pool, tag = (psum_h, "h") if q >= LAST_CHUNK else (psum_f, "f")
                f_banks[q] = pool.tile([P, E], F32, tag=tag, name="f_bank")
            tokens = slice(P * t, P * (t + 1))
            nc.tensor.matmul_mx(
                out=f_banks[q][:],
                lhsT=h_codes[chunk][:, g, tokens].bitcast(FP8X4),
                lhsT_scale=h_scales[chunk][:, g, tokens],
                rhs=w2_codes[:, columns(g)].bitcast(FP8X4),
                rhs_scale=w2_scales[:, columns(g)],
                start=(g == 0),
                stop=(g == PASSES - 1),
            )

        def residual(q):
            bank = psum_aux.tile([P, E], F32, tag="aux", name="r_bank")
            nc.tensor.matmul(out=bank[:], lhsT=ident_bf[:], rhs=y_sb[:, E * q : E * (q + 1)], start=True, stop=False)
            nc.tensor.matmul(out=bank[:], lhsT=ones_bf[:], rhs=b2_row[:], start=False, stop=True)
            resid_banks[q] = bank

        def copy_f(q):
            f_copies[q] = summed_pool.tile([P, E], F32, tag="f_copy", name="f_copy")
            nc.scalar.copy(out=f_copies[q][:], in_=f_banks[q][:])

        def add_on_tensor(q):
            bank = psum_f.tile([P, E], F32, tag="f", name="r_bank")
            nc.tensor.matmul(out=bank[:], lhsT=ident_bf[:], rhs=y_sb[:, E * q : E * (q + 1)], start=True, stop=False)
            nc.tensor.matmul(out=bank[:], lhsT=ones_bf[:], rhs=b2_row[:], start=False, stop=False)
            nc.tensor.matmul(out=bank[:], lhsT=ident[:], rhs=f_copies[q][:], start=False, stop=True)
            summed[q] = bank

        def total(q):
            spare = norm_pool.tile([P, E], BF16, tag="squares", name="spare")
            totals[q] = stat_pool.tile([P, 1], F32, tag="total", name="total")
            nc.scalar.activation(out=spare[:], in_=summed[q][:], func=ACT.Identity, accum_out=totals[q][:])

        def copy_residual(q):
            resid[q] = resid_pool.tile([P, E], F32, tag="resid", name="resid")
            nc.scalar.copy(out=resid[q][:], in_=resid_banks[q][:])

        def add_residual(q):
            summed[q] = summed_pool.tile([P, E], F32, tag="summed", name="summed")
            totals[q] = stat_pool.tile([P, 1], F32, tag="total", name="total")
            nc.vector.scalar_tensor_tensor(
                out=summed[q][:], in0=f_banks[q][:], scalar=1.0, in1=resid[q][:],
                op0=ALU.mult, op1=ALU.add, accum_out=totals[q][:],
            )

        def negative_mean(q):
            neg_mean[q] = stat_pool.tile([P, 1], F32, tag="neg_mean", name="neg_mean")
            nc.vector.tensor_scalar_mul(out=neg_mean[q][:], in0=totals[q][:], scalar1=-1.0 / E)

        def centre(q):
            centred[q] = centred_pool.tile([P, E], F32, tag="centred", name="centred")
            nc.vector.scalar_tensor_tensor(
                out=centred[q][:], in0=summed[q][:], scalar=neg_mean[q][:], in1=gain_bf[:], op0=ALU.add, op1=ALU.mult
            )

        def sum_of_squares(q):
            squares = norm_pool.tile([P, E], BF16, tag="squares", name="squares")
            sums_of_squares[q] = stat_pool.tile([P, 1], F32, tag="sum_squares", name="sum_squares")
            nc.scalar.activation(
                out=squares[:], in_=summed[q][:], func=ACT.Square, bias=neg_mean[q][:], accum_out=sums_of_squares[q][:]
            )

        def inverse_deviation(q):
            padded = stat_pool.tile([P, 1], F32, tag="padded", name="padded")
            nc.scalar.activation(
                out=padded[:], in_=sums_of_squares[q][:], func=ACT.Identity, bias=eps_col[:], scale=1.0 / E
            )
            powers = stat_pool.tile([P, 1], F32, tag="powers", name="powers")
            nc.gpsimd.tensor_tensor(out=powers[:], in0=padded[:], in1=neg_half[:], op=ALU.pow)
            inv_dev[q] = powers[:]

        def scale_shift_store(q):
            ww, c = divmod(q, TILES_PER_CHUNK)
            z = out_pool.tile([P, E], F32, tag="z", name="z")
            nc.vector.scalar_tensor_tensor(
                out=z[:], in0=centred[q][:], scalar=inv_dev[q], in1=shift_bf[:], op0=ALU.mult, op1=ALU.add
            )
            for x in range(2):
                nc.sync.dma_start(out=out_view[ww, c, x], in_=z[x:P:2, :])

        scalar_copy = nc.scalar.copy
        vector_copy = nc.vector.tensor_copy
        f_place, aux_place = (psum_f, "f"), (psum_aux, "aux")

        y_transposes(0, 0, aux_place)
        y_transposes(0, 1, aux_place)
        weight_transposes(0, 0, f_place)
        weight_transposes(0, 1, f_place)
        y_copy(0, 0, scalar_copy)
        y_copy(0, 1, vector_copy)
        weight_copy(0, 0, scalar_copy)
        y_quantise(0)
        weight_quantise_half(0, 0)
        weight_copy(0, 1, scalar_copy)
        weight_quantise_half(0, 1)
        spread_b1()
        gain_bank = spread_row(gain_row)
        shift_bank = spread_row(shift_row)
        scalar_copy(out=gain_bf[:], in_=gain_bank[:])
        vector_copy(out=shift_bf[:], in_=shift_bank[:])
        matmul1_bank(0, 0)
        matmul1_bank(0, 1)
        weight_transposes(1, 0, aux_place)
        weight_transposes(1, 1, aux_place)
        matmul1_bank(0, 2)
        matmul1_bank(0, 3)
        gelu_bank(0, 0)
        gelu_bank(0, 1)
        weight_copy(1, 0, scalar_copy)
        weight_copy(1, 1, vector_copy)
        weight_quantise(1)
        for half in range(2):
            weight_transposes(2, half, f_place)
        for half in range(2):
            weight_transposes(3, half, aux_place)
        gelu_bank(0, 2)
        gelu_bank(0, 3)

        transpose_weights = {0: [(4, f_place)], 1: [(5, f_place), (6, aux_place)], 2: [(7, f_place)]}
        empty_weights = {0: [2, 3], 1: [4], 2: [5, 6], 3: [7]}
        quantise_weights = {1: [2, 3], 2: [4], 3: [5, 6], 4: [7]}
        transpose_y = {0: [(1, 0), (1, 1)]}
        empty_y = {1: [(1, 0), (1, 1)]}
        quantise_y = {2: 1}
        for chunk in range(2, TOKENS // CHUNK):
            for half in range(2):
                transpose_y[PASSES * chunk - 5 + half] = [(chunk, half)]
                empty_y[PASSES * chunk - 4 + half] = [(chunk, half)]
            quantise_y[PASSES * chunk - 2] = chunk

        def tile_at(i, lag):
            return i - lag if 0 <= i - lag < TILES else None

        for i in range(STEPS + SCALE_LAG):
            live = i < STEPS
            last = i == STEPS - 1
            q_resid, q_copy, q_add = tile_at(i, RESIDUAL_LAG), tile_at(i, RESIDUAL_COPY_LAG), tile_at(i, ADD_LAG)
            q_var, q_out = tile_at(i, VARIANCE_LAG), tile_at(i, SCALE_LAG)

            if i == 5:
                load_y_win(4)
            if i in (2, 7, 11):
                load_y({2: 2, 7: 3, 11: 4}[i])

            if 0 < i < STEPS:
                for j in range(PLANES):
                    gelu_bank(i, j)
            if last:
                regroup(i, 1, scalar_copy)
            for n in empty_weights.get(i, []):
                weight_copy(n, 0, scalar_copy)
            for chunk, half in empty_y.get(i, []):
                y_copy(chunk, half, scalar_copy)
            if q_var is not None:
                sum_of_squares(q_var)
            if q_copy is not None and q_copy not in PE_ADDED:
                copy_residual(q_copy)
            if q_var is not None:
                inverse_deviation(q_var)
            if i == STEPS:
                for q in PE_ADDED:
                    copy_f(q)
                for q in PE_ADDED:
                    add_on_tensor(q)
            if q_copy in PE_ADDED:
                total(q_copy)

            for n in empty_weights.get(i, []):
                weight_copy(n, 1, vector_copy)
            for n in quantise_weights.get(i, []):
                weight_quantise(n)
            if i in quantise_y:
                y_quantise(quantise_y[i])
            if live:
                regroup(i, 0, vector_copy)

            for k in range(PLANES):
                if i + 1 < STEPS:
                    matmul1_bank(i + 1, k)
                if q_add is not None and q_add < LAST_CHUNK:
                    matmul2_pass(q_add, k)
            if last:
                for q in range(LAST_CHUNK, TILES):
                    for g in range(PASSES - 1):
                        matmul2_pass(q, g)
            for n, place in transpose_weights.get(i, []):
                for half in range(2):
                    weight_transposes(n, half, place)
            for chunk, half in transpose_y.get(i, []):
                y_transposes(chunk, half, aux_place)
            if q_resid is not None and q_resid not in PE_ADDED:
                residual(q_resid)

            if q_add is not None and q_add not in PE_ADDED:
                add_residual(q_add)
            if live:
                quantise_hidden(i, 0)
            if last:
                for q in range(LAST_CHUNK, LAST_CHUNK + 2):
                    matmul2_pass(q, PASSES - 1)
            if q_add is not None:
                negative_mean(q_add)
            if q_out is not None:
                scale_shift_store(q_out)
            if last:
                quantise_hidden(i, 1)
                for q in range(LAST_CHUNK + 2, TILES):
                    matmul2_pass(q, PASSES - 1)
            if q_add is not None:
                centre(q_add)
